import numpy as np
import ml_dtypes


def mxq(x, axis, fmt="e4m3"):
    dtype, down = {"e4m3": (ml_dtypes.float8_e4m3fn, 7), "e5m2": (ml_dtypes.float8_e5m2, 14)}[fmt]
    v = np.moveaxis(np.asarray(x, np.float32).astype(ml_dtypes.bfloat16).astype(np.float64), axis, -1)
    blocks = v.reshape(v.shape[:-1] + (-1, 32))
    amax = np.abs(blocks).max(-1, keepdims=True)
    byte = np.maximum(np.where(amax > 0, np.frexp(amax)[1] - 1 + 127, 0) - down, 1)
    scale = np.exp2(byte - 127.0)
    codes = (blocks / scale).astype(np.float32).astype(dtype).astype(np.float64)
    return np.moveaxis((codes * scale).reshape(v.shape), -1, axis)


WIDE = False


def mx_kscale(k):
    if not WIDE:
        return np.ones(k)
    levels = np.array([10, -10, 5, -5, 0])
    a = np.random.permutation(np.resize(levels, k // 512 * 4)).reshape(k // 512, 4)
    idx = np.arange(k)
    return np.exp2(a[idx // 512, idx % 128 // 32])


BF16 = ml_dtypes.bfloat16


def bf(x):
    return np.asarray(x, np.float32).astype(BF16)


def f64(x):
    return np.asarray(x).astype(np.float64)


B, CI, CO, H, W = 8, 1024, 512, 32, 32
EPS = 1e-5


def setup_inputs():
    t = mx_kscale(CI)
    return {"x": bf(np.random.standard_normal((B, CI, H, W))),
            "gamma": bf((0.5 + np.random.random(CI)) * t),
            "beta": bf(np.random.standard_normal(CI) * 0.5 * t),
            "running_mean": bf(np.random.standard_normal(CI) * 0.5),
            "running_var": bf(0.5 + np.random.random(CI)),
            "weight": bf(np.random.standard_normal((CO, CI, 1, 1)) * 1.5 / np.sqrt(CI) / t[None, :, None, None])}


def reference(x, gamma, beta, running_mean, running_var, weight):
    x, gamma, beta = f64(x), f64(gamma), f64(beta)
    running_mean, running_var, weight = f64(running_mean), f64(running_var), f64(weight)
    scale = gamma * (1.0 / np.sqrt(running_var + EPS))
    shift = beta - running_mean * scale
    xn = x * scale[None, :, None, None] + shift[None, :, None, None]
    r = np.maximum(xn, 0.0)
    p = r.reshape(B, CI, H // 2, 2, W // 2, 2).mean(axis=(3, 5))
    w2d = weight.reshape(CO, CI)
    pq = mxq(p, 1, "e4m3").reshape(B, CI, (H // 2) * (W // 2))
    y = mxq(w2d, 1, "e4m3") @ pq
    return y.reshape(B, CO, H // 2, W // 2)

@@ -1,0 +1,306 @@
+from contextlib import ExitStack
+
+import concourse.mybir as mybir
+from concourse.masks import make_identity
+
+F32 = mybir.dt.float32
+BF16 = mybir.dt.bfloat16
+U32 = mybir.dt.uint32
+U8 = mybir.dt.uint8
+FP8X4 = mybir.dt.float8_e4m3fn_x4
+ACT = mybir.ActivationFunctionType
+ALU = mybir.AluOpType
+
+P = 128
+B, CI, CO, H, W = 8, 1024, 512, 32, 32
+PIX = (H // 2) * (W // 2)
+PASSES = CI // 512
+MT = CO // P
+EPS = 1e-5
+FLOPS = 2 * B * PIX * CI * CO
+
+ITEMS = [(bt, g, 0, PIX) for bt in range(B - 1) for g in range(PASSES)] + [
+    (B - 1, g, hf * (PIX // 2), PIX // 2) for hf in range(2) for g in range(PASSES)
+]
+VEC_UNITS = [4, 3, 2, 2, 2, 2, 1, 2, 2, 2, 1, 2, 1, 1, 1, 0, 0, 0]
+XB = 10
+RB = 4
+W_AFTER_LOAD = 3
+W_COPY_AFTER = 4
+EVAC_LAG = 6
+
+
+def tile_modelnew_kernel(tc, x, gamma, beta, running_mean, running_var, weight, out):
+    nc = tc.nc
+    n_items = len(ITEMS)
+    with ExitStack() as ctx:
+        const = ctx.enter_context(tc.tile_pool(name="const", bufs=1))
+        xpool = ctx.enter_context(tc.tile_pool(name="xpool", bufs=XB))
+        rpool = ctx.enter_context(tc.tile_pool(name="rpool", bufs=RB))
+        hpool = ctx.enter_context(tc.tile_pool(name="hpool", bufs=2))
+        gpool = ctx.enter_context(tc.tile_pool(name="gpool", bufs=3))
+        cpool = ctx.enter_context(tc.tile_pool(name="cpool", bufs=3))
+        opool = ctx.enter_context(tc.tile_pool(name="opool", bufs=3))
+        psum = ctx.enter_context(tc.psum_pool(name="psum", bufs=8))
+        ctx.enter_context(tc.manual_schedule())
+
+        def load_vec(queue, vec, name):
+            v_sb = const.tile([P, PASSES, 4], BF16, name=name)
+            queue.dma_start(out=v_sb[:], in_=vec.rearrange("(g p t) -> p g t", g=PASSES, t=4))
+            return v_sb
+
+        var_t = load_vec(nc.sync, running_var, "var_t")
+        gam_t = load_vec(nc.scalar, gamma, "gam_t")
+        mean_t = load_vec(nc.sync, running_mean, "mean_t")
+        beta_t = load_vec(nc.scalar, beta, "beta_t")
+
+        xts = {}
+
+        def load(c):
+            bt, g = divmod(c, PASSES)
+            xt = xpool.tile([P, 4, H * W], BF16, name="xt")
+            src = x[bt, g * 512 : (g + 1) * 512].rearrange("(p t) h w -> p t (h w)", t=4)
+            if c == 0:
+                for t in range(4):
+                    nc.sync.dma_start(out=xt[:, t, :], in_=src[:, t, :])
+            else:
+                nc.sync.dma_start(out=xt[:], in_=src)
+            xts[c] = xt
+
+        w_sb = const.tile([P, MT, CI], BF16, name="w_sb")
+        for c in range(XB):
+            load(c)
+            if c == W_AFTER_LOAD:
+                nc.sync.dma_start(out=w_sb[:], in_=weight.rearrange("(m o) k a b -> o m (k a b)", o=P))
+
+        eps_t = const.tile([P, 1], F32, name="eps_t")
+        nc.vector.memset(eps_t[:], EPS)
+        warm = const.tile([P, 1], F32, name="warm")
+        nc.scalar.activation(out=warm[:], in_=eps_t[:], func=ACT.Sqrt)
+        ident = const.tile([P, P], F32, name="ident")
+        make_identity(nc, ident[:])
+        sd = const.tile([P, 8], F32, name="sd")
+        nc.scalar.activation(
+            out=sd[:], in_=var_t[:].rearrange("p g t -> p (g t)"), func=ACT.Sqrt, bias=eps_t[:, 0:1], scale=1.0
+        )
+        rstd = const.tile([P, 8], F32, name="rstd")
+        nc.vector.reciprocal(out=rstd[:], in_=sd[:])
+        sc4 = const.tile([P, 8], F32, name="sc4")
+        nc.vector.scalar_tensor_tensor(
+            out=sc4[:], in0=gam_t[:].rearrange("p g t -> p (g t)"), scalar=0.25, in1=rstd[:], op0=ALU.mult, op1=ALU.mult
+        )
+        ms = const.tile([P, 8], F32, name="ms")
+        nc.vector.tensor_tensor(out=ms[:], in0=mean_t[:].rearrange("p g t -> p (g t)"), in1=sc4[:], op=ALU.mult)
+        sh4 = const.tile([P, 8], F32, name="sh4")
+        nc.vector.scalar_tensor_tensor(
+            out=sh4[:], in0=beta_t[:].rearrange("p g t -> p (g t)"), scalar=0.25, in1=ms[:], op0=ALU.mult, op1=ALU.subtract
+        )
+
+        gw = const.tile([P, PASSES * MT, P, 4], BF16, name="gw", align_bytes=64)
+        wcodes = const.tile([P, PASSES * MT, P], U32, name="wcodes", align_bytes=64)
+        wsc = const.tile([P, PASSES * MT, P], U8, name="wsc", align_bytes=64)
+        wts = []
+
+        def weight_transposes():
+            wf = w_sb[:].bitcast(F32)
+            for k in range(PASSES * MT // 2):
+                wt = psum.tile([P, 2, 2, P], F32, name="wt", tag="bank")
+                for e in range(2):
+                    g, m = divmod(2 * k + e, MT)
+                    for u in range(2):
+                        nc.tensor.transpose(wt[:, e, u, :], wf[:, m, 256 * g + u : 256 * (g + 1) : 2], ident[:])
+                wts.append(wt)
+
+        def weight_copies():
+            gwf = gw[:].bitcast(F32)
+            for k in range(PASSES * MT // 2):
+                nc.scalar.copy(out=gwf[:, 2 * k : 2 * k + 2, :, :], in_=wts[k][:].rearrange("p n u o -> p n o u"))
+
+        def weight_quant():
+            nc.vector.quantize_mx(
+                out=wcodes[:].rearrange("p n o -> p (n o)").bitcast(FP8X4),
+                scales=wsc[:].rearrange("p n o -> p (n o)"),
+                in_=gw[:].rearrange("p n o t -> p (n o t)"),
+            )
+
+        rs = {}
+        hs = {}
+        grps = {}
+        cds = {}
+        accs = {}
+        osbs = {}
+        conv_due = []
+        evac_due = []
+        conv_done = set()
+        evac_done = set()
+
+        def r_tile(k):
+            if k not in rs:
+                rs[k] = rpool.tile([P, 2, 4, 2 * ITEMS[k][3]], F32, name="r")
+            return rs[k]
+
+        def x_view(k):
+            bt, g, p0, npx = ITEMS[k]
+            xv = xts[bt * PASSES + g][:].rearrange("p t (n b) -> p t b n", b=2)
+            return xv[:, :, :, 2 * p0 : 2 * (p0 + npx)]
+
+        def affine_v(k):
+            if k >= n_items:
+                return
+            g = ITEMS[k][1]
+            xv = x_view(k)
+            for t in range(VEC_UNITS[k]):
+                col = 4 * g + t
+                nc.vector.tensor_scalar(
+                    out=r_tile(k)[:, 0, t, :],
+                    in0=xv[:, t, 0, :],
+                    scalar1=sc4[:, col : col + 1],
+                    scalar2=sh4[:, col : col + 1],
+                    op0=ALU.mult,
+                    op1=ALU.add,
+                )
+
+        def affine_s(k):
+            g = ITEMS[k][1]
+            xv = x_view(k)
+            r = r_tile(k)
+            for t in range(4):
+                col = 4 * g + t
+                s_ap = sc4[:, col : col + 1]
+                b_ap = sh4[:, col : col + 1]
+                if t < VEC_UNITS[k]:
+                    nc.scalar.activation(out=r[:, 1, t, :], in_=xv[:, t, 1, :], func=ACT.Relu, bias=b_ap, scale=s_ap)
+                else:
+                    nc.scalar.activation(out=r[:, :, t, :], in_=xv[:, t, :, :], func=ACT.Relu, bias=b_ap, scale=s_ap)
+
+        def add_cols(k):
+            r = rs[k]
+            h = hpool.tile([P, 2, 4, ITEMS[k][3]], F32, name="h")
+            hs[k] = h
+            for a in range(2):
+                nc.vector.scalar_tensor_tensor(
+                    out=h[:, a].rearrange("p t (i w) -> p t i w", w=16),
+                    in0=r[:, 0].rearrange("p t (i a w) -> p a t i w", a=2, w=16)[:, a],
+                    scalar=0.0,
+                    in1=r[:, 1].rearrange("p t (i a w) -> p a t i w", a=2, w=16)[:, a],
+                    op0=ALU.max,
+                    op1=ALU.add,
+                )
+
+        def add_rows(k):
+            h = hs[k]
+            grp = gpool.tile([P, ITEMS[k][3], 4], BF16, name="grp", align_bytes=64)
+            grps[k] = grp
+            nc.vector.tensor_tensor(
+                out=grp[:].rearrange("p (c i) t -> p c t i", i=4),
+                in0=h[:, 0].rearrange("p t (c i) -> p c t i", i=4),
+                in1=h[:, 1].rearrange("p t (c i) -> p c t i", i=4),
+                op=ALU.add,
+            )
+
+        def mx_pass(acc_ap, bt, g, m, p0, npx):
+            codes, scl = cds[bt]
+            nc.tensor.matmul_mx(
+                out=acc_ap,
+                lhsT=wcodes[:, g * MT + m, :].bitcast(FP8X4),
+                lhsT_scale=wsc[:, g * MT + m, :],
+                rhs=codes[:, g, p0 : p0 + npx].bitcast(FP8X4),
+                rhs_scale=scl[:, g, p0 : p0 + npx],
+                start=(g == 0),
+                stop=(g == PASSES - 1),
+            )
+
+        def quant_conv(k):
+            if k < 0:
+                return
+            bt, g, p0, npx = ITEMS[k]
+            if bt not in cds:
+                codes = cpool.tile([P, PASSES, PIX], U32, name="codes", align_bytes=64)
+                scl = cpool.tile([P, PASSES, PIX], U8, name="scl", align_bytes=64)
+                cds[bt] = (codes, scl)
+            codes, scl = cds[bt]
+            nc.vector.quantize_mx(
+                out=codes[:, g, p0 : p0 + npx].bitcast(FP8X4),
+                scales=scl[:, g, p0 : p0 + npx],
+                in_=grps[k][:].rearrange("p x t -> p (x t)"),
+            )
+            if k >= n_items - PASSES:
+                if g == 0:
+                    accs[(bt, p0)] = [psum.tile([P, npx], F32, name="acc%d" % m, tag="bank") for m in range(MT)]
+                for m in range(MT):
+                    mx_pass(accs[(bt, p0)][m][:], bt, g, m, p0, npx)
+            elif g == PASSES - 1:
+                conv_due.append(k)
+
+        def conv(k):
+            bt, g, p0, npx = ITEMS[k]
+            per_bank = 512 // npx
+            banks = []
+            for j in range(MT // per_bank):
+                acc = psum.tile([P, per_bank, npx], F32, name="acc", tag="bank")
+                for e in range(per_bank):
+                    for gg in range(PASSES):
+                        mx_pass(acc[:, e, :], bt, gg, j * per_bank + e, p0, npx)
+                banks.append(acc)
+            accs[(bt, p0)] = banks
+            evac_due.append(k)
+
+        def evacuate(k):
+            bt, g, p0, npx = ITEMS[k]
+            if bt not in osbs:
+                osbs[bt] = opool.tile([P, MT, PIX], F32, name="o_sb")
+            o_sb = osbs[bt]
+            banks = accs[(bt, p0)]
+            dst = out[bt].rearrange("(m o) h w -> o m (h w)", o=P)
+            per_bank = MT // len(banks)
+            if k == n_items - 1:
+                for m in range(MT):
+                    if m < MT // 2:
+                        nc.scalar.copy(out=o_sb[:, m, p0 : p0 + npx], in_=banks[m][:])
+                    else:
+                        nc.vector.tensor_copy(out=o_sb[:, m, p0 : p0 + npx], in_=banks[m][:])
+                for j in range(2):
+                    nc.sync.dma_start(
+                        out=dst[:, 2 * j : 2 * j + 2, p0 : p0 + npx], in_=o_sb[:, 2 * j : 2 * j + 2, p0 : p0 + npx]
+                    )
+            else:
+                for j in range(len(banks)):
+                    nc.scalar.copy(out=o_sb[:, j * per_bank : (j + 1) * per_bank, p0 : p0 + npx], in_=banks[j][:])
+                nc.sync.dma_start(out=dst[:, :, p0 : p0 + npx], in_=o_sb[:, :, p0 : p0 + npx])
+
+        last_item_of_chunk = {}
+        for k in range(n_items):
+            last_item_of_chunk[ITEMS[k][0] * PASSES + ITEMS[k][1]] = k
+
+        def scalar_step(k):
+            affine_s(k)
+            c = ITEMS[k][0] * PASSES + ITEMS[k][1]
+            if last_item_of_chunk[c] == k and c + XB < B * PASSES:
+                load(c + XB)
+            if k == W_COPY_AFTER:
+                weight_copies()
+
+        weight_transposes()
+        affine_v(0)
+        affine_v(1)
+        scalar_step(0)
+        for k in range(n_items):
+            if k + 1 < n_items:
+                scalar_step(k + 1)
+            add_cols(k)
+            quant_conv(k - 1)
+            affine_v(k + 2)
+            add_rows(k)
+            if k == W_COPY_AFTER:
+                weight_quant()
+            if k >= W_COPY_AFTER:
+                for kk in conv_due:
+                    if kk not in conv_done:
+                        conv(kk)
+                        conv_done.add(kk)
+            for kk in evac_due:
+                if kk not in evac_done and (kk + EVAC_LAG - 2 <= k or k + 2 >= n_items):
+                    evacuate(kk)
+                    evac_done.add(kk)
+        quant_conv(n_items - 1)
+        evacuate(n_items - 1)

@@ -22,12 +22,18 @@ FLOPS = 2 * B * PIX * CI * CO
 ITEMS = [(bt, g, 0, PIX) for bt in range(B - 1) for g in range(PASSES)] + [
     (B - 1, g, hf * (PIX // 2), PIX // 2) for hf in range(2) for g in range(PASSES)
 ]
-VEC_UNITS = [4, 3, 2, 2, 2, 2, 1, 2, 2, 2, 1, 2, 1, 1, 1, 0, 0, 0]
-XB = 10
-RB = 4
+KINDS = "VVPVPVPVPVPVPVVVVV"
+VEC_UNITS = [4, 4, 4, 3, 4, 3, 4, 3, 4, 3, 4, 3, 4, 3, 1, 0, 0, 0]
+BACK_ON_VECTOR = []
+XB = 8
+RB = 5
 W_AFTER_LOAD = 3
-W_COPY_AFTER = 4
-EVAC_LAG = 6
+W_T_STEP = 4
+W_COPY_STEP = 5
+L_SUM = 1
+L_ROUND = 3
+L_BACK = 5
+EVAC_LAG = 3
 
 
 def tile_modelnew_kernel(tc, x, gamma, beta, running_mean, running_var, weight, out):
@@ -39,10 +45,14 @@ def tile_modelnew_kernel(tc, x, gamma, beta, running_mean, running_var, weight, 
         rpool = ctx.enter_context(tc.tile_pool(name="rpool", bufs=RB))
         hpool = ctx.enter_context(tc.tile_pool(name="hpool", bufs=2))
         gpool = ctx.enter_context(tc.tile_pool(name="gpool", bufs=3))
-        cpool = ctx.enter_context(tc.tile_pool(name="cpool", bufs=3))
+        cpool = ctx.enter_context(tc.tile_pool(name="cpool", bufs=4))
         opool = ctx.enter_context(tc.tile_pool(name="opool", bufs=3))
+        tpool = ctx.enter_context(tc.tile_pool(name="tpool", bufs=2))
         psum = ctx.enter_context(tc.psum_pool(name="psum", bufs=8))
         ctx.enter_context(tc.manual_schedule())
+
+        def is_kind(k, kind):
+            return 0 <= k < n_items and KINDS[k] == kind
 
         def load_vec(queue, vec, name):
             v_sb = const.tile([P, PASSES, 4], BF16, name=name)
@@ -79,6 +89,8 @@ def tile_modelnew_kernel(tc, x, gamma, beta, running_mean, running_var, weight, 
         nc.scalar.activation(out=warm[:], in_=eps_t[:], func=ACT.Sqrt)
         ident = const.tile([P, P], F32, name="ident")
         make_identity(nc, ident[:])
+        ident_bf = const.tile([P, P], BF16, name="ident_bf")
+        make_identity(nc, ident_bf[:])
         sd = const.tile([P, 8], F32, name="sd")
         nc.scalar.activation(
             out=sd[:], in_=var_t[:].rearrange("p g t -> p (g t)"), func=ACT.Sqrt, bias=eps_t[:, 0:1], scale=1.0
@@ -95,6 +107,23 @@ def tile_modelnew_kernel(tc, x, gamma, beta, running_mean, running_var, weight, 
         nc.vector.scalar_tensor_tensor(
             out=sh4[:], in0=beta_t[:].rearrange("p g t -> p (g t)"), scalar=0.25, in1=ms[:], op0=ALU.mult, op1=ALU.subtract
         )
+        nsh4 = const.tile([P, 8], F32, name="nsh4")
+        nc.vector.tensor_scalar(out=nsh4[:], in0=sh4[:], scalar1=-1.0, scalar2=None, op0=ALU.mult)
+
+        cst = const.tile([P, PASSES, 4, P], F32, name="cst")
+        pscs = []
+
+        def shift_rows_pe():
+            for g in range(PASSES):
+                psc = psum.tile([P, 4, P], F32, name="psc", tag="bank")
+                for t in range(4):
+                    col = 4 * g + t
+                    nc.tensor.transpose(psc[:, t, :], sh4[:, col : col + 1].to_broadcast([P, P]), ident[:])
+                pscs.append(psc)
+
+        def shift_rows_copy():
+            for g in range(PASSES):
+                nc.vector.tensor_scalar(out=cst[:, g], in0=pscs[g][:], scalar1=2.0, scalar2=None, op0=ALU.mult)
 
         gw = const.tile([P, PASSES * MT, P, 4], BF16, name="gw", align_bytes=64)
         wcodes = const.tile([P, PASSES * MT, P], U32, name="wcodes", align_bytes=64)
@@ -129,14 +158,16 @@ def tile_modelnew_kernel(tc, x, gamma, beta, running_mean, running_var, weight, 
         cds = {}
         accs = {}
         osbs = {}
-        conv_due = []
-        evac_due = []
-        conv_done = set()
-        evac_done = set()
+        ps1s = {}
+        ps2s = {}
+        pts = {}
 
         def r_tile(k):
             if k not in rs:
-                rs[k] = rpool.tile([P, 2, 4, 2 * ITEMS[k][3]], F32, name="r")
+                if KINDS[k] == "P":
+                    rs[k] = rpool.tile([P, 2, 2, 4, ITEMS[k][3]], F32, name="r")
+                else:
+                    rs[k] = rpool.tile([P, 2, 4, 2 * ITEMS[k][3]], F32, name="r")
             return rs[k]
 
         def x_view(k):
@@ -144,34 +175,94 @@ def tile_modelnew_kernel(tc, x, gamma, beta, running_mean, running_var, weight, 
             xv = xts[bt * PASSES + g][:].rearrange("p t (n b) -> p t b n", b=2)
             return xv[:, :, :, 2 * p0 : 2 * (p0 + npx)]
 
+        def x_planes(k):
+            bt, g, p0, npx = ITEMS[k]
+            return xts[bt * PASSES + g][:].rearrange("p t (i a w b) -> p t b a i w", a=2, w=16, b=2)
+
         def affine_v(k):
             if k >= n_items:
                 return
             g = ITEMS[k][1]
-            xv = x_view(k)
             for t in range(VEC_UNITS[k]):
                 col = 4 * g + t
-                nc.vector.tensor_scalar(
-                    out=r_tile(k)[:, 0, t, :],
-                    in0=xv[:, t, 0, :],
-                    scalar1=sc4[:, col : col + 1],
-                    scalar2=sh4[:, col : col + 1],
-                    op0=ALU.mult,
-                    op1=ALU.add,
-                )
+                if KINDS[k] == "P":
+                    nc.vector.tensor_scalar(
+                        out=r_tile(k)[:, :, 0, t, :].rearrange("p a (i w) -> p a i w", w=16),
+                        in0=x_planes(k)[:, t, 0],
+                        scalar1=sc4[:, col : col + 1],
+                        scalar2=nsh4[:, col : col + 1],
+                        op0=ALU.mult,
+                        op1=ALU.max,
+                    )
+                else:
+                    nc.vector.tensor_scalar(
+                        out=r_tile(k)[:, 0, t, :],
+                        in0=x_view(k)[:, t, 0, :],
+                        scalar1=sc4[:, col : col + 1],
+                        scalar2=sh4[:, col : col + 1],
+                        op0=ALU.mult,
+                        op1=ALU.add,
+                    )
 
         def affine_s(k):
             g = ITEMS[k][1]
-            xv = x_view(k)
             r = r_tile(k)
             for t in range(4):
                 col = 4 * g + t
                 s_ap = sc4[:, col : col + 1]
                 b_ap = sh4[:, col : col + 1]
-                if t < VEC_UNITS[k]:
-                    nc.scalar.activation(out=r[:, 1, t, :], in_=xv[:, t, 1, :], func=ACT.Relu, bias=b_ap, scale=s_ap)
+                if KINDS[k] == "P":
+                    nc.scalar.activation(
+                        out=r[:, :, 1, t, :].rearrange("p a (i w) -> p a i w", w=16),
+                        in_=x_planes(k)[:, t, 1],
+                        func=ACT.Relu,
+                        bias=b_ap,
+                        scale=s_ap,
+                    )
+                elif t < VEC_UNITS[k]:
+                    nc.scalar.activation(out=r[:, 1, t, :], in_=x_view(k)[:, t, 1, :], func=ACT.Relu, bias=b_ap, scale=s_ap)
                 else:
-                    nc.scalar.activation(out=r[:, :, t, :], in_=xv[:, t, :, :], func=ACT.Relu, bias=b_ap, scale=s_ap)
+                    nc.scalar.activation(out=r[:, :, t, :], in_=x_view(k)[:, t, :, :], func=ACT.Relu, bias=b_ap, scale=s_ap)
+
+        def sum_planes(k):
+            r = rs[k]
+            ps1s[k] = []
+            for hf in range(ITEMS[k][3] // P):
+                ps1 = psum.tile([P, 4, P], F32, name="ps1", tag="bank")
+                for t in range(4):
+                    for q in range(4):
+                        nc.tensor.matmul(
+                            out=ps1[:, t, :],
+                            lhsT=r[:, q % 2, q // 2, t, hf * P : (hf + 1) * P],
+                            rhs=ident[:],
+                            is_transpose=True,
+                            start=(q == 0),
+                            stop=(q == 3),
+                        )
+                ps1s[k].append(ps1)
+
+        def round_sum(k):
+            g = ITEMS[k][1]
+            p_t = tpool.tile([P, ITEMS[k][3] // P, 4, P], BF16, name="p_t")
+            pts[k] = p_t
+            for hf in range(ITEMS[k][3] // P):
+                nc.vector.tensor_tensor(out=p_t[:, hf], in0=ps1s[k][hf][:], in1=cst[:, g], op=ALU.add)
+
+        def turn_back(k):
+            npx = ITEMS[k][3]
+            ps2 = psum.tile([P, 4, npx], BF16, name="ps2", tag="bank")
+            for hf in range(npx // P):
+                for t in range(4):
+                    nc.tensor.transpose(ps2[:, t, hf * P : (hf + 1) * P], pts[k][:, hf, t, :], ident_bf[:])
+            ps2s[k] = ps2
+
+        def copy_back(k):
+            grp = gpool.tile([P, ITEMS[k][3], 4], BF16, name="grp", align_bytes=64)
+            grps[k] = grp
+            if k in BACK_ON_VECTOR:
+                nc.vector.tensor_copy(out=grp[:], in_=ps2s[k][:].rearrange("p t x -> p x t"))
+            else:
+                nc.scalar.copy(out=grp[:], in_=ps2s[k][:].rearrange("p t x -> p x t"))
 
         def add_cols(k):
             r = rs[k]
@@ -210,9 +301,9 @@ def tile_modelnew_kernel(tc, x, gamma, beta, running_mean, running_var, weight, 
                 stop=(g == PASSES - 1),
             )
 
-        def quant_conv(k):
-            if k < 0:
-                return
+        quantised = set()
+
+        def quant(k):
             bt, g, p0, npx = ITEMS[k]
             if bt not in cds:
                 codes = cpool.tile([P, PASSES, PIX], U32, name="codes", align_bytes=64)
@@ -224,13 +315,12 @@ def tile_modelnew_kernel(tc, x, gamma, beta, running_mean, running_var, weight, 
                 scales=scl[:, g, p0 : p0 + npx],
                 in_=grps[k][:].rearrange("p x t -> p (x t)"),
             )
+            quantised.add(k)
             if k >= n_items - PASSES:
                 if g == 0:
                     accs[(bt, p0)] = [psum.tile([P, npx], F32, name="acc%d" % m, tag="bank") for m in range(MT)]
                 for m in range(MT):
                     mx_pass(accs[(bt, p0)][m][:], bt, g, m, p0, npx)
-            elif g == PASSES - 1:
-                conv_due.append(k)
 
         def conv(k):
             bt, g, p0, npx = ITEMS[k]
@@ -243,7 +333,6 @@ def tile_modelnew_kernel(tc, x, gamma, beta, running_mean, running_var, weight, 
                         mx_pass(acc[:, e, :], bt, gg, j * per_bank + e, p0, npx)
                 banks.append(acc)
             accs[(bt, p0)] = banks
-            evac_due.append(k)
 
         def evacuate(k):
             bt, g, p0, npx = ITEMS[k]
@@ -271,36 +360,49 @@ def tile_modelnew_kernel(tc, x, gamma, beta, running_mean, running_var, weight, 
         last_item_of_chunk = {}
         for k in range(n_items):
             last_item_of_chunk[ITEMS[k][0] * PASSES + ITEMS[k][1]] = k
+        closers = [k for k in range(n_items - PASSES) if ITEMS[k][1] == PASSES - 1]
+        conv_step = {}
+        evac_done = set()
 
-        def scalar_step(k):
-            affine_s(k)
-            c = ITEMS[k][0] * PASSES + ITEMS[k][1]
-            if last_item_of_chunk[c] == k and c + XB < B * PASSES:
-                load(c + XB)
-            if k == W_COPY_AFTER:
-                weight_copies()
-
-        weight_transposes()
+        shift_rows_pe()
         affine_v(0)
         affine_v(1)
-        scalar_step(0)
-        for k in range(n_items):
-            if k + 1 < n_items:
-                scalar_step(k + 1)
-            add_cols(k)
-            quant_conv(k - 1)
-            affine_v(k + 2)
-            add_rows(k)
-            if k == W_COPY_AFTER:
+        shift_rows_copy()
+        for j in range(n_items + L_BACK + EVAC_LAG + 2):
+            if j < n_items:
+                affine_s(j)
+                c = ITEMS[j][0] * PASSES + ITEMS[j][1]
+                if last_item_of_chunk[c] == j and c + XB < B * PASSES:
+                    load(c + XB)
+            if j == W_COPY_STEP:
+                weight_copies()
+            if is_kind(j - L_BACK, "P"):
+                copy_back(j - L_BACK)
+            for k in closers:
+                if k in conv_step and k not in evac_done and (j >= conv_step[k] + EVAC_LAG or j >= n_items - 1):
+                    evacuate(k)
+                    evac_done.add(k)
+            if j == W_T_STEP:
+                weight_transposes()
+            if is_kind(j - L_SUM, "P"):
+                sum_planes(j - L_SUM)
+            if is_kind(j - L_ROUND, "P"):
+                round_sum(j - L_ROUND)
+                turn_back(j - L_ROUND)
+            if is_kind(j - 1, "V"):
+                add_cols(j - 1)
+            if is_kind(j - 2, "V"):
+                quant(j - 2)
+            if is_kind(j - L_BACK, "P"):
+                quant(j - L_BACK)
+            affine_v(j + 2)
+            if is_kind(j - 1, "V"):
+                add_rows(j - 1)
+            if j == W_COPY_STEP:
                 weight_quant()
-            if k >= W_COPY_AFTER:
-                for kk in conv_due:
-                    if kk not in conv_done:
-                        conv(kk)
-                        conv_done.add(kk)
-            for kk in evac_due:
-                if kk not in evac_done and (kk + EVAC_LAG - 2 <= k or k + 2 >= n_items):
-                    evacuate(kk)
-                    evac_done.add(kk)
-        quant_conv(n_items - 1)
+            if j >= W_COPY_STEP:
+                for k in closers:
+                    if k not in conv_step and k in quantised and (k - 1) in quantised:
+                        conv(k)
+                        conv_step[k] = j
         evacuate(n_items - 1)

@@ -22,8 +22,8 @@ FLOPS = 2 * B * PIX * CI * CO
 ITEMS = [(bt, g, 0, PIX) for bt in range(B - 1) for g in range(PASSES)] + [
     (B - 1, g, hf * (PIX // 2), PIX // 2) for hf in range(2) for g in range(PASSES)
 ]
-KINDS = "VVPVPVPVPVPVPVVVVV"
-VEC_UNITS = [4, 4, 4, 3, 4, 3, 4, 3, 4, 3, 4, 3, 4, 3, 1, 0, 0, 0]
+KINDS = "VPPPVPPPVPPPPVVVVV"
+VEC_UNITS = [4, 4, 4, 4, 4, 4, 4, 4, 4, 4, 4, 4, 4, 4, 1, 0, 0, 0]
 BACK_ON_VECTOR = []
 XB = 8
 RB = 5
@@ -31,9 +31,10 @@ W_AFTER_LOAD = 3
 W_T_STEP = 4
 W_COPY_STEP = 5
 L_SUM = 1
-L_ROUND = 3
-L_BACK = 5
-EVAC_LAG = 3
+L_ROUND = 2
+L_TURN = 3
+L_BACK = 4
+L_QP = 5
 
 
 def tile_modelnew_kernel(tc, x, gamma, beta, running_mean, running_var, weight, out):
@@ -44,10 +45,10 @@ def tile_modelnew_kernel(tc, x, gamma, beta, running_mean, running_var, weight, 
         xpool = ctx.enter_context(tc.tile_pool(name="xpool", bufs=XB))
         rpool = ctx.enter_context(tc.tile_pool(name="rpool", bufs=RB))
         hpool = ctx.enter_context(tc.tile_pool(name="hpool", bufs=2))
-        gpool = ctx.enter_context(tc.tile_pool(name="gpool", bufs=3))
+        gpool = ctx.enter_context(tc.tile_pool(name="gpool", bufs=4))
         cpool = ctx.enter_context(tc.tile_pool(name="cpool", bufs=4))
         opool = ctx.enter_context(tc.tile_pool(name="opool", bufs=3))
-        tpool = ctx.enter_context(tc.tile_pool(name="tpool", bufs=2))
+        tpool = ctx.enter_context(tc.tile_pool(name="tpool", bufs=3))
         psum = ctx.enter_context(tc.psum_pool(name="psum", bufs=8))
         ctx.enter_context(tc.manual_schedule())
 
@@ -89,8 +90,6 @@ def tile_modelnew_kernel(tc, x, gamma, beta, running_mean, running_var, weight, 
         nc.scalar.activation(out=warm[:], in_=eps_t[:], func=ACT.Sqrt)
         ident = const.tile([P, P], F32, name="ident")
         make_identity(nc, ident[:])
-        ident_bf = const.tile([P, P], BF16, name="ident_bf")
-        make_identity(nc, ident_bf[:])
         sd = const.tile([P, 8], F32, name="sd")
         nc.scalar.activation(
             out=sd[:], in_=var_t[:].rearrange("p g t -> p (g t)"), func=ACT.Sqrt, bias=eps_t[:, 0:1], scale=1.0
@@ -110,7 +109,7 @@ def tile_modelnew_kernel(tc, x, gamma, beta, running_mean, running_var, weight, 
         nsh4 = const.tile([P, 8], F32, name="nsh4")
         nc.vector.tensor_scalar(out=nsh4[:], in0=sh4[:], scalar1=-1.0, scalar2=None, op0=ALU.mult)
 
-        cst = const.tile([P, PASSES, 4, P], F32, name="cst")
+        cst = const.tile([P, PASSES, 2, P, 2], F32, name="cst")
         pscs = []
 
         def shift_rows_pe():
@@ -123,7 +122,9 @@ def tile_modelnew_kernel(tc, x, gamma, beta, running_mean, running_var, weight, 
 
         def shift_rows_copy():
             for g in range(PASSES):
-                nc.vector.tensor_scalar(out=cst[:, g], in0=pscs[g][:], scalar1=2.0, scalar2=None, op0=ALU.mult)
+                nc.vector.tensor_scalar(
+                    out=cst[:, g], in0=pscs[g][:].rearrange("p (u e) c -> p u c e", e=2), scalar1=2.0, scalar2=None, op0=ALU.mult
+                )
 
         gw = const.tile([P, PASSES * MT, P, 4], BF16, name="gw", align_bytes=64)
         wcodes = const.tile([P, PASSES * MT, P], U32, name="wcodes", align_bytes=64)
@@ -243,26 +244,29 @@ def tile_modelnew_kernel(tc, x, gamma, beta, running_mean, running_var, weight, 
 
         def round_sum(k):
             g = ITEMS[k][1]
-            p_t = tpool.tile([P, ITEMS[k][3] // P, 4, P], BF16, name="p_t")
+            p_t = tpool.tile([P, ITEMS[k][3] // P, 2, P, 2], BF16, name="p_t")
             pts[k] = p_t
             for hf in range(ITEMS[k][3] // P):
-                nc.vector.tensor_tensor(out=p_t[:, hf], in0=ps1s[k][hf][:], in1=cst[:, g], op=ALU.add)
+                nc.vector.tensor_tensor(
+                    out=p_t[:, hf], in0=ps1s[k][hf][:].rearrange("p (u e) c -> p u c e", e=2), in1=cst[:, g], op=ALU.add
+                )
 
         def turn_back(k):
             npx = ITEMS[k][3]
-            ps2 = psum.tile([P, 4, npx], BF16, name="ps2", tag="bank")
+            ps2 = psum.tile([P, 2, npx], F32, name="ps2", tag="bank")
+            ptw = pts[k][:].rearrange("p h u c e -> p h u (c e)").bitcast(F32)
             for hf in range(npx // P):
-                for t in range(4):
-                    nc.tensor.transpose(ps2[:, t, hf * P : (hf + 1) * P], pts[k][:, hf, t, :], ident_bf[:])
+                for u in range(2):
+                    nc.tensor.transpose(ps2[:, u, hf * P : (hf + 1) * P], ptw[:, hf, u, :], ident[:])
             ps2s[k] = ps2
 
         def copy_back(k):
             grp = gpool.tile([P, ITEMS[k][3], 4], BF16, name="grp", align_bytes=64)
             grps[k] = grp
             if k in BACK_ON_VECTOR:
-                nc.vector.tensor_copy(out=grp[:], in_=ps2s[k][:].rearrange("p t x -> p x t"))
+                nc.vector.tensor_copy(out=grp[:].bitcast(F32), in_=ps2s[k][:].rearrange("p u x -> p x u"))
             else:
-                nc.scalar.copy(out=grp[:], in_=ps2s[k][:].rearrange("p t x -> p x t"))
+                nc.scalar.copy(out=grp[:].bitcast(F32), in_=ps2s[k][:].rearrange("p u x -> p x u"))
 
         def add_cols(k):
             r = rs[k]
@@ -368,7 +372,8 @@ def tile_modelnew_kernel(tc, x, gamma, beta, running_mean, running_var, weight, 
         affine_v(0)
         affine_v(1)
         shift_rows_copy()
-        for j in range(n_items + L_BACK + EVAC_LAG + 2):
+        quant_step = {}
+        for j in range(n_items + L_QP + 4):
             if j < n_items:
                 affine_s(j)
                 c = ITEMS[j][0] * PASSES + ITEMS[j][1]
@@ -379,22 +384,25 @@ def tile_modelnew_kernel(tc, x, gamma, beta, running_mean, running_var, weight, 
             if is_kind(j - L_BACK, "P"):
                 copy_back(j - L_BACK)
             for k in closers:
-                if k in conv_step and k not in evac_done and (j >= conv_step[k] + EVAC_LAG or j >= n_items - 1):
+                if k in conv_step and k not in evac_done and j > conv_step[k]:
                     evacuate(k)
                     evac_done.add(k)
             if j == W_T_STEP:
                 weight_transposes()
-            if is_kind(j - L_SUM, "P"):
-                sum_planes(j - L_SUM)
             if is_kind(j - L_ROUND, "P"):
                 round_sum(j - L_ROUND)
-                turn_back(j - L_ROUND)
+            if is_kind(j - L_SUM, "P"):
+                sum_planes(j - L_SUM)
+            if is_kind(j - L_TURN, "P"):
+                turn_back(j - L_TURN)
             if is_kind(j - 1, "V"):
                 add_cols(j - 1)
             if is_kind(j - 2, "V"):
                 quant(j - 2)
-            if is_kind(j - L_BACK, "P"):
-                quant(j - L_BACK)
+                quant_step[j - 2] = j
+            if is_kind(j - L_QP, "P"):
+                quant(j - L_QP)
+                quant_step[j - L_QP] = j
             affine_v(j + 2)
             if is_kind(j - 1, "V"):
                 add_rows(j - 1)
@@ -402,7 +410,9 @@ def tile_modelnew_kernel(tc, x, gamma, beta, running_mean, running_var, weight, 
                 weight_quant()
             if j >= W_COPY_STEP:
                 for k in closers:
+                    late = j >= n_items - 1
                     if k not in conv_step and k in quantised and (k - 1) in quantised:
-                        conv(k)
-                        conv_step[k] = j
+                        if late or (quant_step[k] < j and quant_step[k - 1] < j and j not in conv_step.values()):
+                            conv(k)
+                            conv_step[k] = j
         evacuate(n_items - 1)

@@ -397,13 +397,13 @@ def tile_modelnew_kernel(tc, x, gamma, beta, running_mean, running_var, weight, 
                 turn_back(j - L_TURN)
             if is_kind(j - 1, "V"):
                 add_cols(j - 1)
-            if is_kind(j - 2, "V"):
-                quant(j - 2)
-                quant_step[j - 2] = j
             if is_kind(j - L_QP, "P"):
                 quant(j - L_QP)
                 quant_step[j - L_QP] = j
             affine_v(j + 2)
+            if is_kind(j - 2, "V"):
+                quant(j - 2)
+                quant_step[j - 2] = j
             if is_kind(j - 1, "V"):
                 add_rows(j - 1)
             if j == W_COPY_STEP:

@@ -22,19 +22,22 @@ FLOPS = 2 * B * PIX * CI * CO
 ITEMS = [(bt, g, 0, PIX) for bt in range(B - 1) for g in range(PASSES)] + [
     (B - 1, g, hf * (PIX // 2), PIX // 2) for hf in range(2) for g in range(PASSES)
 ]
-KINDS = "VPPPVPPPVPPPPVVVVV"
-VEC_UNITS = [4, 4, 4, 4, 4, 4, 4, 4, 4, 4, 4, 4, 4, 4, 1, 0, 0, 0]
-BACK_ON_VECTOR = []
+VEC_T = [4] * (2 * (B - 1)) + [4, 4, 4, 4]
+KINDS = ["01"[k % 2] == "1" and "PV" or "PP" for k in range(2 * (B - 1))] + ["P","P","P","V"]
 XB = 8
 RB = 5
-W_AFTER_LOAD = 3
-W_T_STEP = 4
-W_COPY_STEP = 5
+CB = 4
+W_AFTER_LOAD = 4
+W_PIECE = 2
+W_T_STEP = 5
+W_COPY_STEP = 6
 L_SUM = 1
 L_ROUND = 2
 L_TURN = 3
 L_BACK = 4
 L_QP = 5
+L_QV = 2
+AHEAD = 1
 
 
 def tile_modelnew_kernel(tc, x, gamma, beta, running_mean, running_var, weight, out):
@@ -45,15 +48,15 @@ def tile_modelnew_kernel(tc, x, gamma, beta, running_mean, running_var, weight, 
         xpool = ctx.enter_context(tc.tile_pool(name="xpool", bufs=XB))
         rpool = ctx.enter_context(tc.tile_pool(name="rpool", bufs=RB))
         hpool = ctx.enter_context(tc.tile_pool(name="hpool", bufs=2))
-        gpool = ctx.enter_context(tc.tile_pool(name="gpool", bufs=4))
-        cpool = ctx.enter_context(tc.tile_pool(name="cpool", bufs=4))
+        gpool = ctx.enter_context(tc.tile_pool(name="gpool", bufs=6))
+        cpool = ctx.enter_context(tc.tile_pool(name="cpool", bufs=CB))
         opool = ctx.enter_context(tc.tile_pool(name="opool", bufs=3))
         tpool = ctx.enter_context(tc.tile_pool(name="tpool", bufs=3))
         psum = ctx.enter_context(tc.psum_pool(name="psum", bufs=8))
         ctx.enter_context(tc.manual_schedule())
 
-        def is_kind(k, kind):
-            return 0 <= k < n_items and KINDS[k] == kind
+        def halves(k, kind):
+            return [hf for hf in range(len(KINDS[k])) if KINDS[k][hf] == kind] if 0 <= k < n_items else []
 
         def load_vec(queue, vec, name):
             v_sb = const.tile([P, PASSES, 4], BF16, name=name)
@@ -79,10 +82,12 @@ def tile_modelnew_kernel(tc, x, gamma, beta, running_mean, running_var, weight, 
             xts[c] = xt
 
         w_sb = const.tile([P, MT, CI], BF16, name="w_sb")
+        w_src = weight.rearrange("(m o) k a b -> o m (k a b)", o=P)
         for c in range(XB):
             load(c)
-            if c == W_AFTER_LOAD:
-                nc.sync.dma_start(out=w_sb[:], in_=weight.rearrange("(m o) k a b -> o m (k a b)", o=P))
+            if 0 <= c - W_AFTER_LOAD < MT // W_PIECE:
+                m0 = W_PIECE * (c - W_AFTER_LOAD)
+                nc.sync.dma_start(out=w_sb[:, m0 : m0 + W_PIECE], in_=w_src[:, m0 : m0 + W_PIECE])
 
         eps_t = const.tile([P, 1], F32, name="eps_t")
         nc.vector.memset(eps_t[:], EPS)
@@ -163,72 +168,52 @@ def tile_modelnew_kernel(tc, x, gamma, beta, running_mean, running_var, weight, 
         ps2s = {}
         pts = {}
 
+        def due(j, lag, kind):
+            return [k for k in range(n_items) if j == k + lag and halves(k, kind)]
+
         def r_tile(k):
             if k not in rs:
-                if KINDS[k] == "P":
-                    rs[k] = rpool.tile([P, 2, 2, 4, ITEMS[k][3]], F32, name="r")
-                else:
-                    rs[k] = rpool.tile([P, 2, 4, 2 * ITEMS[k][3]], F32, name="r")
+                rs[k] = rpool.tile([P, 2, 2, 4, ITEMS[k][3]], F32, name="r")
             return rs[k]
 
-        def x_view(k):
+        def x_planes(k, t, b):
             bt, g, p0, npx = ITEMS[k]
-            xv = xts[bt * PASSES + g][:].rearrange("p t (n b) -> p t b n", b=2)
-            return xv[:, :, :, 2 * p0 : 2 * (p0 + npx)]
+            xv = xts[bt * PASSES + g][:].rearrange("p t (i a w b) -> p t b a i w", a=2, w=16, b=2)
+            return xv[:, t, b, :, p0 // 16 : (p0 + npx) // 16, :]
 
-        def x_planes(k):
-            bt, g, p0, npx = ITEMS[k]
-            return xts[bt * PASSES + g][:].rearrange("p t (i a w b) -> p t b a i w", a=2, w=16, b=2)
+        def r_planes(k, t, b):
+            return r_tile(k)[:, :, b, t, :].rearrange("p a (i w) -> p a i w", w=16)
 
         def affine_v(k):
             if k >= n_items:
                 return
-            g = ITEMS[k][1]
-            for t in range(VEC_UNITS[k]):
-                col = 4 * g + t
-                if KINDS[k] == "P":
-                    nc.vector.tensor_scalar(
-                        out=r_tile(k)[:, :, 0, t, :].rearrange("p a (i w) -> p a i w", w=16),
-                        in0=x_planes(k)[:, t, 0],
-                        scalar1=sc4[:, col : col + 1],
-                        scalar2=nsh4[:, col : col + 1],
-                        op0=ALU.mult,
-                        op1=ALU.max,
-                    )
-                else:
-                    nc.vector.tensor_scalar(
-                        out=r_tile(k)[:, 0, t, :],
-                        in0=x_view(k)[:, t, 0, :],
-                        scalar1=sc4[:, col : col + 1],
-                        scalar2=sh4[:, col : col + 1],
-                        op0=ALU.mult,
-                        op1=ALU.add,
-                    )
+            for t in range(VEC_T[k]):
+                col = 4 * ITEMS[k][1] + t
+                nc.vector.tensor_scalar(
+                    out=r_planes(k, t, 0),
+                    in0=x_planes(k, t, 0),
+                    scalar1=sc4[:, col : col + 1],
+                    scalar2=nsh4[:, col : col + 1],
+                    op0=ALU.mult,
+                    op1=ALU.max,
+                )
 
         def affine_s(k):
-            g = ITEMS[k][1]
-            r = r_tile(k)
             for t in range(4):
-                col = 4 * g + t
-                s_ap = sc4[:, col : col + 1]
-                b_ap = sh4[:, col : col + 1]
-                if KINDS[k] == "P":
+                col = 4 * ITEMS[k][1] + t
+                for b in range(t < VEC_T[k], 2):
                     nc.scalar.activation(
-                        out=r[:, :, 1, t, :].rearrange("p a (i w) -> p a i w", w=16),
-                        in_=x_planes(k)[:, t, 1],
+                        out=r_planes(k, t, b),
+                        in_=x_planes(k, t, b),
                         func=ACT.Relu,
-                        bias=b_ap,
-                        scale=s_ap,
+                        bias=sh4[:, col : col + 1],
+                        scale=sc4[:, col : col + 1],
                     )
-                elif t < VEC_UNITS[k]:
-                    nc.scalar.activation(out=r[:, 1, t, :], in_=x_view(k)[:, t, 1, :], func=ACT.Relu, bias=b_ap, scale=s_ap)
-                else:
-                    nc.scalar.activation(out=r[:, :, t, :], in_=x_view(k)[:, t, :, :], func=ACT.Relu, bias=b_ap, scale=s_ap)
 
         def sum_planes(k):
             r = rs[k]
-            ps1s[k] = []
-            for hf in range(ITEMS[k][3] // P):
+            ps1s[k] = {}
+            for hf in halves(k, "P"):
                 ps1 = psum.tile([P, 4, P], F32, name="ps1", tag="bank")
                 for t in range(4):
                     for q in range(4):
@@ -240,60 +225,69 @@ def tile_modelnew_kernel(tc, x, gamma, beta, running_mean, running_var, weight, 
                             start=(q == 0),
                             stop=(q == 3),
                         )
-                ps1s[k].append(ps1)
+                ps1s[k][hf] = ps1
 
         def round_sum(k):
             g = ITEMS[k][1]
-            p_t = tpool.tile([P, ITEMS[k][3] // P, 2, P, 2], BF16, name="p_t")
+            p_t = tpool.tile([P, 2, 2, P, 2], BF16, name="p_t")
             pts[k] = p_t
-            for hf in range(ITEMS[k][3] // P):
-                nc.vector.tensor_tensor(
-                    out=p_t[:, hf], in0=ps1s[k][hf][:].rearrange("p (u e) c -> p u c e", e=2), in1=cst[:, g], op=ALU.add
-                )
+            for hf in halves(k, "P"):
+                sums = ps1s[k][hf][:].rearrange("p (u e) c -> p u c e", e=2)
+                if VEC_T[k]:
+                    nc.vector.tensor_tensor(out=p_t[:, hf], in0=sums, in1=cst[:, g], op=ALU.add)
+                else:
+                    nc.vector.tensor_copy(out=p_t[:, hf], in_=sums)
 
         def turn_back(k):
-            npx = ITEMS[k][3]
-            ps2 = psum.tile([P, 2, npx], F32, name="ps2", tag="bank")
+            ps2 = psum.tile([P, 2, 2 * P], F32, name="ps2", tag="bank")
             ptw = pts[k][:].rearrange("p h u c e -> p h u (c e)").bitcast(F32)
-            for hf in range(npx // P):
+            for hf in halves(k, "P"):
                 for u in range(2):
                     nc.tensor.transpose(ps2[:, u, hf * P : (hf + 1) * P], ptw[:, hf, u, :], ident[:])
             ps2s[k] = ps2
 
+        def g_tile(k):
+            if k not in grps:
+                grps[k] = gpool.tile([P, ITEMS[k][3], 4], BF16, name="grp", align_bytes=64)
+            return grps[k]
+
         def copy_back(k):
-            grp = gpool.tile([P, ITEMS[k][3], 4], BF16, name="grp", align_bytes=64)
-            grps[k] = grp
-            if k in BACK_ON_VECTOR:
-                nc.vector.tensor_copy(out=grp[:].bitcast(F32), in_=ps2s[k][:].rearrange("p u x -> p x u"))
-            else:
-                nc.scalar.copy(out=grp[:].bitcast(F32), in_=ps2s[k][:].rearrange("p u x -> p x u"))
+            hs_p = halves(k, "P")
+            lo, hi = hs_p[0] * P, (hs_p[-1] + 1) * P
+            nc.scalar.copy(out=g_tile(k)[:, lo:hi, :].bitcast(F32), in_=ps2s[k][:, :, lo:hi].rearrange("p u x -> p x u"))
 
         def add_cols(k):
             r = rs[k]
-            h = hpool.tile([P, 2, 4, ITEMS[k][3]], F32, name="h")
+            h = hpool.tile([P, 2, 4, P], F32, name="h")
             hs[k] = h
-            for a in range(2):
+            hf = halves(k, "V")[0]
+            px = slice(hf * P, (hf + 1) * P)
+            if not VEC_T[k]:
+                for a in range(2):
+                    nc.vector.tensor_tensor(out=h[:, a], in0=r[:, a, 0, :, px], in1=r[:, a, 1, :, px], op=ALU.add)
+                return
+            for t in range(4):
+                col = 4 * ITEMS[k][1] + t
                 nc.vector.scalar_tensor_tensor(
-                    out=h[:, a].rearrange("p t (i w) -> p t i w", w=16),
-                    in0=r[:, 0].rearrange("p t (i a w) -> p a t i w", a=2, w=16)[:, a],
-                    scalar=0.0,
-                    in1=r[:, 1].rearrange("p t (i a w) -> p a t i w", a=2, w=16)[:, a],
-                    op0=ALU.max,
+                    out=h[:, :, t, :],
+                    in0=r[:, :, 0, t, px],
+                    scalar=sh4[:, col : col + 1],
+                    in1=r[:, :, 1, t, px],
+                    op0=ALU.add,
                     op1=ALU.add,
                 )
 
         def add_rows(k):
             h = hs[k]
-            grp = gpool.tile([P, ITEMS[k][3], 4], BF16, name="grp", align_bytes=64)
-            grps[k] = grp
+            hf = halves(k, "V")[0]
             nc.vector.tensor_tensor(
-                out=grp[:].rearrange("p (c i) t -> p c t i", i=4),
+                out=g_tile(k)[:, hf * P : (hf + 1) * P, :].rearrange("p (c i) t -> p c t i", i=4),
                 in0=h[:, 0].rearrange("p t (c i) -> p c t i", i=4),
                 in1=h[:, 1].rearrange("p t (c i) -> p c t i", i=4),
                 op=ALU.add,
             )
 
-        def mx_pass(acc_ap, bt, g, m, p0, npx):
+        def mx_pass(acc_ap, bt, g, m, p0, npx, start, stop):
             codes, scl = cds[bt]
             nc.tensor.matmul_mx(
                 out=acc_ap,
@@ -301,8 +295,8 @@ def tile_modelnew_kernel(tc, x, gamma, beta, running_mean, running_var, weight, 
                 lhsT_scale=wsc[:, g * MT + m, :],
                 rhs=codes[:, g, p0 : p0 + npx].bitcast(FP8X4),
                 rhs_scale=scl[:, g, p0 : p0 + npx],
-                start=(g == 0),
-                stop=(g == PASSES - 1),
+                start=start,
+                stop=stop,
             )
 
         quantised = set()
@@ -321,10 +315,11 @@ def tile_modelnew_kernel(tc, x, gamma, beta, running_mean, running_var, weight, 
             )
             quantised.add(k)
             if k >= n_items - PASSES:
-                if g == 0:
+                first = (bt, p0) not in accs
+                if first:
                     accs[(bt, p0)] = [psum.tile([P, npx], F32, name="acc%d" % m, tag="bank") for m in range(MT)]
                 for m in range(MT):
-                    mx_pass(accs[(bt, p0)][m][:], bt, g, m, p0, npx)
+                    mx_pass(accs[(bt, p0)][m][:], bt, g, m, p0, npx, first, not first)
 
         def conv(k):
             bt, g, p0, npx = ITEMS[k]
@@ -334,7 +329,7 @@ def tile_modelnew_kernel(tc, x, gamma, beta, running_mean, running_var, weight, 
                 acc = psum.tile([P, per_bank, npx], F32, name="acc", tag="bank")
                 for e in range(per_bank):
                     for gg in range(PASSES):
-                        mx_pass(acc[:, e, :], bt, gg, j * per_bank + e, p0, npx)
+                        mx_pass(acc[:, e, :], bt, gg, j * per_bank + e, p0, npx, gg == 0, gg == PASSES - 1)
                 banks.append(acc)
             accs[(bt, p0)] = banks
 
@@ -358,7 +353,11 @@ def tile_modelnew_kernel(tc, x, gamma, beta, running_mean, running_var, weight, 
                     )
             else:
                 for j in range(len(banks)):
-                    nc.scalar.copy(out=o_sb[:, j * per_bank : (j + 1) * per_bank, p0 : p0 + npx], in_=banks[j][:])
+                    dst_sb = o_sb[:, j * per_bank : (j + 1) * per_bank, p0 : p0 + npx]
+                    if k == n_items - 3:
+                        nc.vector.tensor_copy(out=dst_sb, in_=banks[j][:])
+                    else:
+                        nc.scalar.copy(out=dst_sb, in_=banks[j][:])
                 nc.sync.dma_start(out=dst[:, :, p0 : p0 + npx], in_=o_sb[:, :, p0 : p0 + npx])
 
         last_item_of_chunk = {}
@@ -369,43 +368,46 @@ def tile_modelnew_kernel(tc, x, gamma, beta, running_mean, running_var, weight, 
         evac_done = set()
 
         shift_rows_pe()
-        affine_v(0)
-        affine_v(1)
+        for k in range(AHEAD):
+            affine_v(k)
         shift_rows_copy()
         quant_step = {}
-        for j in range(n_items + L_QP + 4):
-            if j < n_items:
-                affine_s(j)
-                c = ITEMS[j][0] * PASSES + ITEMS[j][1]
-                if last_item_of_chunk[c] == j and c + XB < B * PASSES:
-                    load(c + XB)
+        for j in range(n_items):
+            affine_s(j)
+            c = ITEMS[j][0] * PASSES + ITEMS[j][1]
+            if last_item_of_chunk[c] == j and c + XB < B * PASSES:
+                load(c + XB)
             if j == W_COPY_STEP:
                 weight_copies()
-            if is_kind(j - L_BACK, "P"):
-                copy_back(j - L_BACK)
+            if j == W_T_STEP:
+                weight_transposes()
+            for k in due(j, L_ROUND, "P"):
+                round_sum(k)
+            for k in due(j, L_SUM, "P"):
+                sum_planes(k)
+            for k in due(j, L_TURN, "P"):
+                turn_back(k)
+            for k in due(j, L_BACK, "P"):
+                copy_back(k)
             for k in closers:
                 if k in conv_step and k not in evac_done and j > conv_step[k]:
                     evacuate(k)
                     evac_done.add(k)
-            if j == W_T_STEP:
-                weight_transposes()
-            if is_kind(j - L_ROUND, "P"):
-                round_sum(j - L_ROUND)
-            if is_kind(j - L_SUM, "P"):
-                sum_planes(j - L_SUM)
-            if is_kind(j - L_TURN, "P"):
-                turn_back(j - L_TURN)
-            if is_kind(j - 1, "V"):
-                add_cols(j - 1)
-            if is_kind(j - L_QP, "P"):
-                quant(j - L_QP)
-                quant_step[j - L_QP] = j
-            affine_v(j + 2)
-            if is_kind(j - 2, "V"):
-                quant(j - 2)
-                quant_step[j - 2] = j
-            if is_kind(j - 1, "V"):
-                add_rows(j - 1)
+            for k in due(j, 1, "V"):
+                add_cols(k)
+            for k in due(j, L_QP, "P"):
+                quant(k)
+                quant_step[k] = j
+            if AHEAD == 2:
+                affine_v(j + 2)
+            for k in due(j, L_QV, "V"):
+                if not halves(k, "P"):
+                    quant(k)
+                    quant_step[k] = j
+            for k in due(j, 1, "V"):
+                add_rows(k)
+            if AHEAD == 1:
+                affine_v(j + 1)
             if j == W_COPY_STEP:
                 weight_quant()
             if j >= W_COPY_STEP:
@@ -415,4 +417,22 @@ def tile_modelnew_kernel(tc, x, gamma, beta, running_mean, running_var, weight, 
                         if late or (quant_step[k] < j and quant_step[k - 1] < j and j not in conv_step.values()):
                             conv(k)
                             conv_step[k] = j
-        evacuate(n_items - 1)
+        turn_back(15)
+        copy_back(14)
+        evacuate(11)
+        quant(13)
+        round_sum(16)
+        copy_back(15)
+        turn_back(16)
+        conv(13)
+        copy_back(16)
+        quant(14)
+        add_cols(17)
+        quant(15)
+        evacuate(13)
+        conv(15)
+        add_rows(17)
+        quant(16)
+        quant(17)
+        evacuate(15)
+        evacuate(17)

@@ -22,11 +22,12 @@ FLOPS = 2 * B * PIX * CI * CO
 ITEMS = [(bt, g, 0, PIX) for bt in range(B - 1) for g in range(PASSES)] + [
     (B - 1, g, hf * (PIX // 2), PIX // 2) for hf in range(2) for g in range(PASSES)
 ]
-VEC_T = [4] * (2 * (B - 1)) + [4, 4, 4, 4]
-KINDS = ["01"[k % 2] == "1" and "PV" or "PP" for k in range(2 * (B - 1))] + ["P","P","P","V"]
+VEC_T = [3,4,4,3,4,4,3,4,4,3,4,4,3,4,4,4,4,4]
+KINDS = ["PV","PV","PP","PV","PV","PP","PV","PV","PP","PV","PV","PP","PV","PV","P","P","P","V"]
 XB = 8
 RB = 5
 CB = 4
+W_FIRST = False
 W_AFTER_LOAD = 4
 W_PIECE = 2
 W_T_STEP = 5
@@ -114,7 +115,7 @@ def tile_modelnew_kernel(tc, x, gamma, beta, running_mean, running_var, weight, 
         nsh4 = const.tile([P, 8], F32, name="nsh4")
         nc.vector.tensor_scalar(out=nsh4[:], in0=sh4[:], scalar1=-1.0, scalar2=None, op0=ALU.mult)
 
-        cst = const.tile([P, PASSES, 2, P, 2], F32, name="cst")
+        csts = {nv: const.tile([P, PASSES, 2, P, 2], F32, name="cst%d" % nv) for nv in sorted(set(VEC_T)) if nv}
         pscs = []
 
         def shift_rows_pe():
@@ -126,10 +127,13 @@ def tile_modelnew_kernel(tc, x, gamma, beta, running_mean, running_var, weight, 
                 pscs.append(psc)
 
         def shift_rows_copy():
-            for g in range(PASSES):
-                nc.vector.tensor_scalar(
-                    out=cst[:, g], in0=pscs[g][:].rearrange("p (u e) c -> p u c e", e=2), scalar1=2.0, scalar2=None, op0=ALU.mult
-                )
+            for nv in csts:
+                for g in range(PASSES):
+                    nc.vector.tensor_scalar(
+                        out=csts[nv][:, g], in0=pscs[g][:].rearrange("p (u e) c -> p u c e", e=2), scalar1=2.0, scalar2=None, op0=ALU.mult
+                    )
+                for t in range(nv, 4):
+                    nc.vector.memset(csts[nv][:, :, t // 2, :, t % 2], 0.0)
 
         gw = const.tile([P, PASSES * MT, P, 4], BF16, name="gw", align_bytes=64)
         wcodes = const.tile([P, PASSES * MT, P], U32, name="wcodes", align_bytes=64)
@@ -234,7 +238,7 @@ def tile_modelnew_kernel(tc, x, gamma, beta, running_mean, running_var, weight, 
             for hf in halves(k, "P"):
                 sums = ps1s[k][hf][:].rearrange("p (u e) c -> p u c e", e=2)
                 if VEC_T[k]:
-                    nc.vector.tensor_tensor(out=p_t[:, hf], in0=sums, in1=cst[:, g], op=ALU.add)
+                    nc.vector.tensor_tensor(out=p_t[:, hf], in0=sums, in1=csts[VEC_T[k]][:, g], op=ALU.add)
                 else:
                     nc.vector.tensor_copy(out=p_t[:, hf], in_=sums)
 
@@ -256,12 +260,14 @@ def tile_modelnew_kernel(tc, x, gamma, beta, running_mean, running_var, weight, 
             lo, hi = hs_p[0] * P, (hs_p[-1] + 1) * P
             nc.scalar.copy(out=g_tile(k)[:, lo:hi, :].bitcast(F32), in_=ps2s[k][:, :, lo:hi].rearrange("p u x -> p x u"))
 
+        def v_run(k):
+            return slice(halves(k, "V")[0] * P, (halves(k, "V")[-1] + 1) * P)
+
         def add_cols(k):
             r = rs[k]
-            h = hpool.tile([P, 2, 4, P], F32, name="h")
+            px = v_run(k)
+            h = hpool.tile([P, 2, 4, px.stop - px.start], F32, name="h")
             hs[k] = h
-            hf = halves(k, "V")[0]
-            px = slice(hf * P, (hf + 1) * P)
             if not VEC_T[k]:
                 for a in range(2):
                     nc.vector.tensor_tensor(out=h[:, a], in0=r[:, a, 0, :, px], in1=r[:, a, 1, :, px], op=ALU.add)
@@ -271,7 +277,7 @@ def tile_modelnew_kernel(tc, x, gamma, beta, running_mean, running_var, weight, 
                 nc.vector.scalar_tensor_tensor(
                     out=h[:, :, t, :],
                     in0=r[:, :, 0, t, px],
-                    scalar=sh4[:, col : col + 1],
+                    scalar=sh4[:, col : col + 1] if t < VEC_T[k] else 0.0,
                     in1=r[:, :, 1, t, px],
                     op0=ALU.add,
                     op1=ALU.add,
@@ -279,9 +285,8 @@ def tile_modelnew_kernel(tc, x, gamma, beta, running_mean, running_var, weight, 
 
         def add_rows(k):
             h = hs[k]
-            hf = halves(k, "V")[0]
             nc.vector.tensor_tensor(
-                out=g_tile(k)[:, hf * P : (hf + 1) * P, :].rearrange("p (c i) t -> p c t i", i=4),
+                out=g_tile(k)[:, v_run(k), :].rearrange("p (c i) t -> p c t i", i=4),
                 in0=h[:, 0].rearrange("p t (c i) -> p c t i", i=4),
                 in1=h[:, 1].rearrange("p t (c i) -> p c t i", i=4),
                 op=ALU.add,
@@ -373,11 +378,13 @@ def tile_modelnew_kernel(tc, x, gamma, beta, running_mean, running_var, weight, 
         shift_rows_copy()
         quant_step = {}
         for j in range(n_items):
+            if j == W_COPY_STEP and W_FIRST:
+                weight_copies()
             affine_s(j)
             c = ITEMS[j][0] * PASSES + ITEMS[j][1]
             if last_item_of_chunk[c] == j and c + XB < B * PASSES:
                 load(c + XB)
-            if j == W_COPY_STEP:
+            if j == W_COPY_STEP and not W_FIRST:
                 weight_copies()
             if j == W_T_STEP:
                 weight_transposes()

@@ -22,7 +22,7 @@ FLOPS = 2 * B * PIX * CI * CO
 ITEMS = [(bt, g, 0, PIX) for bt in range(B - 1) for g in range(PASSES)] + [
     (B - 1, g, hf * (PIX // 2), PIX // 2) for hf in range(2) for g in range(PASSES)
 ]
-VEC_T = [3,4,4,3,4,4,3,4,4,3,4,4,3,4,4,4,4,4]
+S_EXTRA = [1,1,0,1,1,0,1,1,0,1,1,0,1,1,0,0,0,0]
 KINDS = ["PV","PV","PP","PV","PV","PP","PV","PV","PP","PV","PV","PP","PV","PV","P","P","P","V"]
 XB = 8
 RB = 5
@@ -39,6 +39,7 @@ L_BACK = 4
 L_QP = 5
 L_QV = 2
 AHEAD = 1
+CST_ON_SCALAR = True
 
 
 def tile_modelnew_kernel(tc, x, gamma, beta, running_mean, running_var, weight, out):
@@ -96,26 +97,34 @@ def tile_modelnew_kernel(tc, x, gamma, beta, running_mean, running_var, weight, 
         nc.scalar.activation(out=warm[:], in_=eps_t[:], func=ACT.Sqrt)
         ident = const.tile([P, P], F32, name="ident")
         make_identity(nc, ident[:])
-        sd = const.tile([P, 8], F32, name="sd")
-        nc.scalar.activation(
-            out=sd[:], in_=var_t[:].rearrange("p g t -> p (g t)"), func=ACT.Sqrt, bias=eps_t[:, 0:1], scale=1.0
+
+        def columns(tile):
+            return tile[:].rearrange("p g t -> p (g t)")
+
+        gm4 = const.tile([P, 8], F32, name="gm4")
+        nc.vector.scalar_tensor_tensor(
+            out=gm4[:], in0=columns(gam_t), scalar=0.25, in1=columns(mean_t), op0=ALU.mult, op1=ALU.mult
         )
+        sd = const.tile([P, 8], F32, name="sd")
+        nc.scalar.activation(out=sd[:], in_=columns(var_t), func=ACT.Sqrt, bias=eps_t[:, 0:1], scale=1.0)
         rstd = const.tile([P, 8], F32, name="rstd")
         nc.vector.reciprocal(out=rstd[:], in_=sd[:])
+        ms = const.tile([P, 8], F32, name="ms")
+        nc.vector.tensor_tensor(out=ms[:], in0=gm4[:], in1=rstd[:], op=ALU.mult)
         sc4 = const.tile([P, 8], F32, name="sc4")
         nc.vector.scalar_tensor_tensor(
-            out=sc4[:], in0=gam_t[:].rearrange("p g t -> p (g t)"), scalar=0.25, in1=rstd[:], op0=ALU.mult, op1=ALU.mult
+            out=sc4[:], in0=columns(gam_t), scalar=0.25, in1=rstd[:], op0=ALU.mult, op1=ALU.mult
         )
-        ms = const.tile([P, 8], F32, name="ms")
-        nc.vector.tensor_tensor(out=ms[:], in0=mean_t[:].rearrange("p g t -> p (g t)"), in1=sc4[:], op=ALU.mult)
         sh4 = const.tile([P, 8], F32, name="sh4")
         nc.vector.scalar_tensor_tensor(
-            out=sh4[:], in0=beta_t[:].rearrange("p g t -> p (g t)"), scalar=0.25, in1=ms[:], op0=ALU.mult, op1=ALU.subtract
+            out=sh4[:], in0=columns(beta_t), scalar=0.25, in1=ms[:], op0=ALU.mult, op1=ALU.subtract
         )
         nsh4 = const.tile([P, 8], F32, name="nsh4")
-        nc.vector.tensor_scalar(out=nsh4[:], in0=sh4[:], scalar1=-1.0, scalar2=None, op0=ALU.mult)
+        nc.vector.scalar_tensor_tensor(
+            out=nsh4[:], in0=columns(beta_t), scalar=-0.25, in1=ms[:], op0=ALU.mult, op1=ALU.add
+        )
 
-        csts = {nv: const.tile([P, PASSES, 2, P, 2], F32, name="cst%d" % nv) for nv in sorted(set(VEC_T)) if nv}
+        cst = const.tile([P, PASSES, 2, P, 2], F32, name="cst")
         pscs = []
 
         def shift_rows_pe():
@@ -127,13 +136,12 @@ def tile_modelnew_kernel(tc, x, gamma, beta, running_mean, running_var, weight, 
                 pscs.append(psc)
 
         def shift_rows_copy():
-            for nv in csts:
-                for g in range(PASSES):
-                    nc.vector.tensor_scalar(
-                        out=csts[nv][:, g], in0=pscs[g][:].rearrange("p (u e) c -> p u c e", e=2), scalar1=2.0, scalar2=None, op0=ALU.mult
-                    )
-                for t in range(nv, 4):
-                    nc.vector.memset(csts[nv][:, :, t // 2, :, t % 2], 0.0)
+            for g in range(PASSES):
+                src = pscs[g][:].rearrange("p (u e) c -> p u c e", e=2)
+                if CST_ON_SCALAR:
+                    nc.scalar.activation(out=cst[:, g], in_=src, func=ACT.Copy, scale=2.0)
+                else:
+                    nc.vector.tensor_scalar(out=cst[:, g], in0=src, scalar1=2.0, scalar2=None, op0=ALU.mult)
 
         gw = const.tile([P, PASSES * MT, P, 4], BF16, name="gw", align_bytes=64)
         wcodes = const.tile([P, PASSES * MT, P], U32, name="wcodes", align_bytes=64)
@@ -180,22 +188,30 @@ def tile_modelnew_kernel(tc, x, gamma, beta, running_mean, running_var, weight, 
                 rs[k] = rpool.tile([P, 2, 2, 4, ITEMS[k][3]], F32, name="r")
             return rs[k]
 
-        def x_planes(k, t, b):
+        def x_planes(k, t, b, lo, hi):
             bt, g, p0, npx = ITEMS[k]
             xv = xts[bt * PASSES + g][:].rearrange("p t (i a w b) -> p t b a i w", a=2, w=16, b=2)
-            return xv[:, t, b, :, p0 // 16 : (p0 + npx) // 16, :]
+            return xv[:, t, b, :, (p0 + lo) // 16 : (p0 + hi) // 16, :]
 
-        def r_planes(k, t, b):
-            return r_tile(k)[:, :, b, t, :].rearrange("p a (i w) -> p a i w", w=16)
+        def r_planes(k, t, b, lo, hi):
+            return r_tile(k)[:, :, b, t, lo:hi].rearrange("p a (i w) -> p a i w", w=16)
+
+        def vector_end(k, t):
+            if t < 4 - S_EXTRA[k]:
+                return ITEMS[k][3]
+            return v_run(k).start
 
         def affine_v(k):
             if k >= n_items:
                 return
-            for t in range(VEC_T[k]):
+            for t in range(4):
+                end = vector_end(k, t)
+                if end == 0:
+                    continue
                 col = 4 * ITEMS[k][1] + t
                 nc.vector.tensor_scalar(
-                    out=r_planes(k, t, 0),
-                    in0=x_planes(k, t, 0),
+                    out=r_planes(k, t, 0, 0, end),
+                    in0=x_planes(k, t, 0, 0, end),
                     scalar1=sc4[:, col : col + 1],
                     scalar2=nsh4[:, col : col + 1],
                     op0=ALU.mult,
@@ -205,10 +221,13 @@ def tile_modelnew_kernel(tc, x, gamma, beta, running_mean, running_var, weight, 
         def affine_s(k):
             for t in range(4):
                 col = 4 * ITEMS[k][1] + t
-                for b in range(t < VEC_T[k], 2):
+                for b in range(2):
+                    lo, hi = vector_end(k, t) if b == 0 else 0, ITEMS[k][3]
+                    if lo == hi:
+                        continue
                     nc.scalar.activation(
-                        out=r_planes(k, t, b),
-                        in_=x_planes(k, t, b),
+                        out=r_planes(k, t, b, lo, hi),
+                        in_=x_planes(k, t, b, lo, hi),
                         func=ACT.Relu,
                         bias=sh4[:, col : col + 1],
                         scale=sc4[:, col : col + 1],
@@ -237,10 +256,7 @@ def tile_modelnew_kernel(tc, x, gamma, beta, running_mean, running_var, weight, 
             pts[k] = p_t
             for hf in halves(k, "P"):
                 sums = ps1s[k][hf][:].rearrange("p (u e) c -> p u c e", e=2)
-                if VEC_T[k]:
-                    nc.vector.tensor_tensor(out=p_t[:, hf], in0=sums, in1=csts[VEC_T[k]][:, g], op=ALU.add)
-                else:
-                    nc.vector.tensor_copy(out=p_t[:, hf], in_=sums)
+                nc.vector.tensor_tensor(out=p_t[:, hf], in0=sums, in1=cst[:, g], op=ALU.add)
 
         def turn_back(k):
             ps2 = psum.tile([P, 2, 2 * P], F32, name="ps2", tag="bank")
@@ -268,16 +284,12 @@ def tile_modelnew_kernel(tc, x, gamma, beta, running_mean, running_var, weight, 
             px = v_run(k)
             h = hpool.tile([P, 2, 4, px.stop - px.start], F32, name="h")
             hs[k] = h
-            if not VEC_T[k]:
-                for a in range(2):
-                    nc.vector.tensor_tensor(out=h[:, a], in0=r[:, a, 0, :, px], in1=r[:, a, 1, :, px], op=ALU.add)
-                return
             for t in range(4):
                 col = 4 * ITEMS[k][1] + t
                 nc.vector.scalar_tensor_tensor(
                     out=h[:, :, t, :],
                     in0=r[:, :, 0, t, px],
-                    scalar=sh4[:, col : col + 1] if t < VEC_T[k] else 0.0,
+                    scalar=sh4[:, col : col + 1] if t < 4 - S_EXTRA[k] else 0.0,
                     in1=r[:, :, 1, t, px],
                     op0=ALU.add,
                     op1=ALU.add,
@@ -375,12 +387,15 @@ def tile_modelnew_kernel(tc, x, gamma, beta, running_mean, running_var, weight, 
         shift_rows_pe()
         for k in range(AHEAD):
             affine_v(k)
-        shift_rows_copy()
+        if not CST_ON_SCALAR:
+            shift_rows_copy()
         quant_step = {}
         for j in range(n_items):
             if j == W_COPY_STEP and W_FIRST:
                 weight_copies()
             affine_s(j)
+            if CST_ON_SCALAR and j == 0:
+                shift_rows_copy()
             c = ITEMS[j][0] * PASSES + ITEMS[j][1]
             if last_item_of_chunk[c] == j and c + XB < B * PASSES:
                 load(c + XB)

@@ -22,8 +22,8 @@ FLOPS = 2 * B * PIX * CI * CO
 ITEMS = [(bt, g, 0, PIX) for bt in range(B - 1) for g in range(PASSES)] + [
     (B - 1, g, hf * (PIX // 2), PIX // 2) for hf in range(2) for g in range(PASSES)
 ]
-S_EXTRA = [1,1,0,1,1,0,1,1,0,1,1,0,1,1,0,0,0,0]
-KINDS = ["PV","PV","PP","PV","PV","PP","PV","PV","PP","PV","PV","PP","PV","PV","P","P","P","V"]
+S_EXTRA = [1,1,0,1,1,0,1,1,0,0,0,0,0,0,0,0,0,0]
+KINDS = ["PV","PV","PP","PV","PV","PP","PV","PV","PP","PV","PP","PV","PP","PV","P","P","P","V"]
 XB = 8
 RB = 5
 CB = 4
@@ -284,7 +284,7 @@ def tile_modelnew_kernel(tc, x, gamma, beta, running_mean, running_var, weight, 
             px = v_run(k)
             h = hpool.tile([P, 2, 4, px.stop - px.start], F32, name="h")
             hs[k] = h
-            for t in range(4):
+            for t in range(4) if k == n_items - 1 else reversed(range(4)):
                 col = 4 * ITEMS[k][1] + t
                 nc.vector.scalar_tensor_tensor(
                     out=h[:, :, t, :],

@@ -74,7 +74,7 @@ def tile_modelnew_kernel(tc, x, gamma, beta, running_mean, running_var, weight, 
 
         def load(c):
             bt, g = divmod(c, PASSES)
-            xt = xpool.tile([P, 4, H * W], BF16, name="xt")
+            xt = xpool.tile([P, 4, H * W], BF16, name="xt", align_bytes=256)
             src = x[bt, g * 512 : (g + 1) * 512].rearrange("(p t) h w -> p t (h w)", t=4)
             if c == 0:
                 for t in range(4):
@@ -83,7 +83,7 @@ def tile_modelnew_kernel(tc, x, gamma, beta, running_mean, running_var, weight, 
                 nc.sync.dma_start(out=xt[:], in_=src)
             xts[c] = xt
 
-        w_sb = const.tile([P, MT, CI], BF16, name="w_sb")
+        w_sb = const.tile([P, MT, CI], BF16, name="w_sb", align_bytes=256)
         w_src = weight.rearrange("(m o) k a b -> o m (k a b)", o=P)
         for c in range(XB):
             load(c)
@@ -95,7 +95,7 @@ def tile_modelnew_kernel(tc, x, gamma, beta, running_mean, running_var, weight, 
         nc.vector.memset(eps_t[:], EPS)
         warm = const.tile([P, 1], F32, name="warm")
         nc.scalar.activation(out=warm[:], in_=eps_t[:], func=ACT.Sqrt)
-        ident = const.tile([P, P], F32, name="ident")
+        ident = const.tile([P, P], F32, name="ident", align_bytes=256)
         make_identity(nc, ident[:])
 
         def columns(tile):
@@ -124,7 +124,7 @@ def tile_modelnew_kernel(tc, x, gamma, beta, running_mean, running_var, weight, 
             out=nsh4[:], in0=columns(beta_t), scalar=-0.25, in1=ms[:], op0=ALU.mult, op1=ALU.add
         )
 
-        cst = const.tile([P, PASSES, 2, P, 2], F32, name="cst")
+        cst = const.tile([P, PASSES, 2, P, 2], F32, name="cst", align_bytes=256)
         pscs = []
 
         def shift_rows_pe():
@@ -143,9 +143,9 @@ def tile_modelnew_kernel(tc, x, gamma, beta, running_mean, running_var, weight, 
                 else:
                     nc.vector.tensor_scalar(out=cst[:, g], in0=src, scalar1=2.0, scalar2=None, op0=ALU.mult)
 
-        gw = const.tile([P, PASSES * MT, P, 4], BF16, name="gw", align_bytes=64)
-        wcodes = const.tile([P, PASSES * MT, P], U32, name="wcodes", align_bytes=64)
-        wsc = const.tile([P, PASSES * MT, P], U8, name="wsc", align_bytes=64)
+        gw = const.tile([P, PASSES * MT, P, 4], BF16, name="gw", align_bytes=256)
+        wcodes = const.tile([P, PASSES * MT, P], U32, name="wcodes", align_bytes=256)
+        wsc = const.tile([P, PASSES * MT, P], U8, name="wsc", align_bytes=256)
         wts = []
 
         def weight_transposes():
@@ -185,7 +185,7 @@ def tile_modelnew_kernel(tc, x, gamma, beta, running_mean, running_var, weight, 
 
         def r_tile(k):
             if k not in rs:
-                rs[k] = rpool.tile([P, 2, 2, 4, ITEMS[k][3]], F32, name="r")
+                rs[k] = rpool.tile([P, 2, 2, 4, ITEMS[k][3]], F32, name="r", align_bytes=256)
             return rs[k]
 
         def x_planes(k, t, b, lo, hi):
@@ -252,7 +252,7 @@ def tile_modelnew_kernel(tc, x, gamma, beta, running_mean, running_var, weight, 
 
         def round_sum(k):
             g = ITEMS[k][1]
-            p_t = tpool.tile([P, 2, 2, P, 2], BF16, name="p_t")
+            p_t = tpool.tile([P, 2, 2, P, 2], BF16, name="p_t", align_bytes=256)
             pts[k] = p_t
             for hf in halves(k, "P"):
                 sums = ps1s[k][hf][:].rearrange("p (u e) c -> p u c e", e=2)
@@ -268,7 +268,7 @@ def tile_modelnew_kernel(tc, x, gamma, beta, running_mean, running_var, weight, 
 
         def g_tile(k):
             if k not in grps:
-                grps[k] = gpool.tile([P, ITEMS[k][3], 4], BF16, name="grp", align_bytes=64)
+                grps[k] = gpool.tile([P, ITEMS[k][3], 4], BF16, name="grp", align_bytes=256)
             return grps[k]
 
         def copy_back(k):
@@ -282,7 +282,7 @@ def tile_modelnew_kernel(tc, x, gamma, beta, running_mean, running_var, weight, 
         def add_cols(k):
             r = rs[k]
             px = v_run(k)
-            h = hpool.tile([P, 2, 4, px.stop - px.start], F32, name="h")
+            h = hpool.tile([P, 2, 4, px.stop - px.start], F32, name="h", align_bytes=256)
             hs[k] = h
             for t in range(4) if k == n_items - 1 else reversed(range(4)):
                 col = 4 * ITEMS[k][1] + t
@@ -321,8 +321,8 @@ def tile_modelnew_kernel(tc, x, gamma, beta, running_mean, running_var, weight, 
         def quant(k):
             bt, g, p0, npx = ITEMS[k]
             if bt not in cds:
-                codes = cpool.tile([P, PASSES, PIX], U32, name="codes", align_bytes=64)
-                scl = cpool.tile([P, PASSES, PIX], U8, name="scl", align_bytes=64)
+                codes = cpool.tile([P, PASSES, PIX], U32, name="codes", align_bytes=256)
+                scl = cpool.tile([P, PASSES, PIX], U8, name="scl", align_bytes=256)
                 cds[bt] = (codes, scl)
             codes, scl = cds[bt]
             nc.vector.quantize_mx(
@@ -353,7 +353,7 @@ def tile_modelnew_kernel(tc, x, gamma, beta, running_mean, running_var, weight, 
         def evacuate(k):
             bt, g, p0, npx = ITEMS[k]
             if bt not in osbs:
-                osbs[bt] = opool.tile([P, MT, PIX], F32, name="o_sb")
+                osbs[bt] = opool.tile([P, MT, PIX], F32, name="o_sb", align_bytes=256)
             o_sb = osbs[bt]
             banks = accs[(bt, p0)]
             dst = out[bt].rearrange("(m o) h w -> o m (h w)", o=P)

@@ -39,6 +39,8 @@ L_BACK = 4
 L_QP = 5
 L_QV = 2
 AHEAD = 1
+SPLIT_STORE = 9
+SAME_STEP = 99
 CST_ON_SCALAR = True
 
 
@@ -84,7 +86,7 @@ def tile_modelnew_kernel(tc, x, gamma, beta, running_mean, running_var, weight, 
             xts[c] = xt
 
         w_sb = const.tile([P, MT, CI], BF16, name="w_sb", align_bytes=256)
-        w_src = weight.rearrange("(m o) k a b -> o m (k a b)", o=P)
+        w_src = weight.rearrange("(o m) k a b -> o m (k a b)", o=P)
         for c in range(XB):
             load(c)
             if 0 <= c - W_AFTER_LOAD < MT // W_PIECE:
@@ -356,7 +358,7 @@ def tile_modelnew_kernel(tc, x, gamma, beta, running_mean, running_var, weight, 
                 osbs[bt] = opool.tile([P, MT, PIX], F32, name="o_sb", align_bytes=256)
             o_sb = osbs[bt]
             banks = accs[(bt, p0)]
-            dst = out[bt].rearrange("(m o) h w -> o m (h w)", o=P)
+            dst = out[bt].rearrange("(o m) h w -> o m (h w)", o=P)
             per_bank = MT // len(banks)
             if k == n_items - 1:
                 for m in range(MT):
@@ -375,7 +377,11 @@ def tile_modelnew_kernel(tc, x, gamma, beta, running_mean, running_var, weight, 
                         nc.vector.tensor_copy(out=dst_sb, in_=banks[j][:])
                     else:
                         nc.scalar.copy(out=dst_sb, in_=banks[j][:])
-                nc.sync.dma_start(out=dst[:, :, p0 : p0 + npx], in_=o_sb[:, :, p0 : p0 + npx])
+                    if k >= SPLIT_STORE:
+                        ms = slice(j * per_bank, (j + 1) * per_bank)
+                        nc.sync.dma_start(out=dst[:, ms, p0 : p0 + npx], in_=o_sb[:, ms, p0 : p0 + npx])
+                if k < SPLIT_STORE:
+                    nc.sync.dma_start(out=dst[:, :, p0 : p0 + npx], in_=o_sb[:, :, p0 : p0 + npx])
 
         last_item_of_chunk = {}
         for k in range(n_items):
@@ -434,9 +440,8 @@ def tile_modelnew_kernel(tc, x, gamma, beta, running_mean, running_var, weight, 
                 weight_quant()
             if j >= W_COPY_STEP:
                 for k in closers:
-                    late = j >= n_items - 1
                     if k not in conv_step and k in quantised and (k - 1) in quantised:
-                        if late or (quant_step[k] < j and quant_step[k - 1] < j and j not in conv_step.values()):
+                        if quant_step[k] < j + (k >= SAME_STEP) and quant_step[k - 1] < j and j not in conv_step.values():
                             conv(k)
                             conv_step[k] = j
         turn_back(15)

from contextlib import ExitStack

import concourse.mybir as mybir
from concourse.masks import make_identity

F32 = mybir.dt.float32
BF16 = mybir.dt.bfloat16
U32 = mybir.dt.uint32
U8 = mybir.dt.uint8
FP8X4 = mybir.dt.float8_e4m3fn_x4
ACT = mybir.ActivationFunctionType
ALU = mybir.AluOpType

P = 128
B, CI, CO, H, W = 8, 1024, 512, 32, 32
PIX = (H // 2) * (W // 2)
PASSES = CI // 512
MT = CO // P
EPS = 1e-5
FLOPS = 2 * B * PIX * CI * CO

ITEMS = [(bt, g, 0, PIX) for bt in range(B - 1) for g in range(PASSES)] + [
    (B - 1, g, hf * (PIX // 2), PIX // 2) for hf in range(2) for g in range(PASSES)
]
S_EXTRA = [1,1,0,1,1,0,1,1,0,0,0,0,0,0,0,0,0,0]
KINDS = ["PV","PV","PP","PV","PV","PP","PV","PV","PP","PV","PP","PV","PP","PV","P","P","P","V"]
XB = 8
RB = 5
CB = 4
W_FIRST = False
W_AFTER_LOAD = 4
W_PIECE = 2
W_T_STEP = 5
W_COPY_STEP = 6
L_SUM = 1
L_ROUND = 2
L_TURN = 3
L_BACK = 4
L_QP = 5
L_QV = 2
AHEAD = 1
SPLIT_STORE = 9
SAME_STEP = 99
CST_ON_SCALAR = True


def tile_modelnew_kernel(tc, x, gamma, beta, running_mean, running_var, weight, out):
    nc = tc.nc
    n_items = len(ITEMS)
    with ExitStack() as ctx:
        const = ctx.enter_context(tc.tile_pool(name="const", bufs=1))
        xpool = ctx.enter_context(tc.tile_pool(name="xpool", bufs=XB))
        rpool = ctx.enter_context(tc.tile_pool(name="rpool", bufs=RB))
        hpool = ctx.enter_context(tc.tile_pool(name="hpool", bufs=2))
        gpool = ctx.enter_context(tc.tile_pool(name="gpool", bufs=6))
        cpool = ctx.enter_context(tc.tile_pool(name="cpool", bufs=CB))
        opool = ctx.enter_context(tc.tile_pool(name="opool", bufs=3))
        tpool = ctx.enter_context(tc.tile_pool(name="tpool", bufs=3))
        psum = ctx.enter_context(tc.psum_pool(name="psum", bufs=8))
        ctx.enter_context(tc.manual_schedule())

        def halves(k, kind):
            return [hf for hf in range(len(KINDS[k])) if KINDS[k][hf] == kind] if 0 <= k < n_items else []

        def load_vec(queue, vec, name):
            v_sb = const.tile([P, PASSES, 4], BF16, name=name)
            queue.dma_start(out=v_sb[:], in_=vec.rearrange("(g p t) -> p g t", g=PASSES, t=4))
            return v_sb

        var_t = load_vec(nc.sync, running_var, "var_t")
        gam_t = load_vec(nc.scalar, gamma, "gam_t")
        mean_t = load_vec(nc.sync, running_mean, "mean_t")
        beta_t = load_vec(nc.scalar, beta, "beta_t")

        xts = {}

        def load(c):
            bt, g = divmod(c, PASSES)
            xt = xpool.tile([P, 4, H * W], BF16, name="xt", align_bytes=256)
            src = x[bt, g * 512 : (g + 1) * 512].rearrange("(p t) h w -> p t (h w)", t=4)
            if c == 0:
                for t in range(4):
                    nc.sync.dma_start(out=xt[:, t, :], in_=src[:, t, :])
            else:
                nc.sync.dma_start(out=xt[:], in_=src)
            xts[c] = xt

        w_sb = const.tile([P, MT, CI], BF16, name="w_sb", align_bytes=256)
        w_src = weight.rearrange("(o m) k a b -> o m (k a b)", o=P)
        for c in range(XB):
            load(c)
            if 0 <= c - W_AFTER_LOAD < MT // W_PIECE:
                m0 = W_PIECE * (c - W_AFTER_LOAD)
                nc.sync.dma_start(out=w_sb[:, m0 : m0 + W_PIECE], in_=w_src[:, m0 : m0 + W_PIECE])

        eps_t = const.tile([P, 1], F32, name="eps_t")
        nc.vector.memset(eps_t[:], EPS)
        warm = const.tile([P, 1], F32, name="warm")
        nc.scalar.activation(out=warm[:], in_=eps_t[:], func=ACT.Sqrt)
        ident = const.tile([P, P], F32, name="ident", align_bytes=256)
        make_identity(nc, ident[:])

        def columns(tile):
            return tile[:].rearrange("p g t -> p (g t)")

        gm4 = const.tile([P, 8], F32, name="gm4")
        nc.vector.scalar_tensor_tensor(
            out=gm4[:], in0=columns(gam_t), scalar=0.25, in1=columns(mean_t), op0=ALU.mult, op1=ALU.mult
        )
        sd = const.tile([P, 8], F32, name="sd")
        nc.scalar.activation(out=sd[:], in_=columns(var_t), func=ACT.Sqrt, bias=eps_t[:, 0:1], scale=1.0)
        rstd = const.tile([P, 8], F32, name="rstd")
        nc.vector.reciprocal(out=rstd[:], in_=sd[:])
        ms = const.tile([P, 8], F32, name="ms")
        nc.vector.tensor_tensor(out=ms[:], in0=gm4[:], in1=rstd[:], op=ALU.mult)
        sc4 = const.tile([P, 8], F32, name="sc4")
        nc.vector.scalar_tensor_tensor(
            out=sc4[:], in0=columns(gam_t), scalar=0.25, in1=rstd[:], op0=ALU.mult, op1=ALU.mult
        )
        sh4 = const.tile([P, 8], F32, name="sh4")
        nc.vector.scalar_tensor_tensor(
            out=sh4[:], in0=columns(beta_t), scalar=0.25, in1=ms[:], op0=ALU.mult, op1=ALU.subtract
        )
        nsh4 = const.tile([P, 8], F32, name="nsh4")
        nc.vector.scalar_tensor_tensor(
            out=nsh4[:], in0=columns(beta_t), scalar=-0.25, in1=ms[:], op0=ALU.mult, op1=ALU.add
        )

        cst = const.tile([P, PASSES, 2, P, 2], F32, name="cst", align_bytes=256)
        pscs = []

        def shift_rows_pe():
            for g in range(PASSES):
                psc = psum.tile([P, 4, P], F32, name="psc", tag="bank")
                for t in range(4):
                    col = 4 * g + t
                    nc.tensor.transpose(psc[:, t, :], sh4[:, col : col + 1].to_broadcast([P, P]), ident[:])
                pscs.append(psc)

        def shift_rows_copy():
            for g in range(PASSES):
                src = pscs[g][:].rearrange("p (u e) c -> p u c e", e=2)
                if CST_ON_SCALAR:
                    nc.scalar.activation(out=cst[:, g], in_=src, func=ACT.Copy, scale=2.0)
                else:
                    nc.vector.tensor_scalar(out=cst[:, g], in0=src, scalar1=2.0, scalar2=None, op0=ALU.mult)

        gw = const.tile([P, PASSES * MT, P, 4], BF16, name="gw", align_bytes=256)
        wcodes = const.tile([P, PASSES * MT, P], U32, name="wcodes", align_bytes=256)
        wsc = const.tile([P, PASSES * MT, P], U8, name="wsc", align_bytes=256)
        wts = []

        def weight_transposes():
            wf = w_sb[:].bitcast(F32)
            for k in range(PASSES * MT // 2):
                wt = psum.tile([P, 2, 2, P], F32, name="wt", tag="bank")
                for e in range(2):
                    g, m = divmod(2 * k + e, MT)
                    for u in range(2):
                        nc.tensor.transpose(wt[:, e, u, :], wf[:, m, 256 * g + u : 256 * (g + 1) : 2], ident[:])
                wts.append(wt)

        def weight_copies():
            gwf = gw[:].bitcast(F32)
            for k in range(PASSES * MT // 2):
                nc.scalar.copy(out=gwf[:, 2 * k : 2 * k + 2, :, :], in_=wts[k][:].rearrange("p n u o -> p n o u"))

        def weight_quant():
            nc.vector.quantize_mx(
                out=wcodes[:].rearrange("p n o -> p (n o)").bitcast(FP8X4),
                scales=wsc[:].rearrange("p n o -> p (n o)"),
                in_=gw[:].rearrange("p n o t -> p (n o t)"),
            )

        rs = {}
        hs = {}
        grps = {}
        cds = {}
        accs = {}
        osbs = {}
        ps1s = {}
        ps2s = {}
        pts = {}

        def due(j, lag, kind):
            return [k for k in range(n_items) if j == k + lag and halves(k, kind)]

        def r_tile(k):
            if k not in rs:
                rs[k] = rpool.tile([P, 2, 2, 4, ITEMS[k][3]], F32, name="r", align_bytes=256)
            return rs[k]

        def x_planes(k, t, b, lo, hi):
            bt, g, p0, npx = ITEMS[k]
            xv = xts[bt * PASSES + g][:].rearrange("p t (i a w b) -> p t b a i w", a=2, w=16, b=2)
            return xv[:, t, b, :, (p0 + lo) // 16 : (p0 + hi) // 16, :]

        def r_planes(k, t, b, lo, hi):
            return r_tile(k)[:, :, b, t, lo:hi].rearrange("p a (i w) -> p a i w", w=16)

        def vector_end(k, t):
            if t < 4 - S_EXTRA[k]:
                return ITEMS[k][3]
            return v_run(k).start

        def affine_v(k):
            if k >= n_items:
                return
            for t in range(4):
                end = vector_end(k, t)
                if end == 0:
                    continue
                col = 4 * ITEMS[k][1] + t
                nc.vector.tensor_scalar(
                    out=r_planes(k, t, 0, 0, end),
                    in0=x_planes(k, t, 0, 0, end),
                    scalar1=sc4[:, col : col + 1],
                    scalar2=nsh4[:, col : col + 1],
                    op0=ALU.mult,
                    op1=ALU.max,
                )

        def affine_s(k):
            for t in range(4):
                col = 4 * ITEMS[k][1] + t
                for b in range(2):
                    lo, hi = vector_end(k, t) if b == 0 else 0, ITEMS[k][3]
                    if lo == hi:
                        continue
                    nc.scalar.activation(
                        out=r_planes(k, t, b, lo, hi),
                        in_=x_planes(k, t, b, lo, hi),
                        func=ACT.Relu,
                        bias=sh4[:, col : col + 1],
                        scale=sc4[:, col : col + 1],
                    )

        def sum_planes(k):
            r = rs[k]
            ps1s[k] = {}
            for hf in halves(k, "P"):
                ps1 = psum.tile([P, 4, P], F32, name="ps1", tag="bank")
                for t in range(4):
                    for q in range(4):
                        nc.tensor.matmul(
                            out=ps1[:, t, :],
                            lhsT=r[:, q % 2, q // 2, t, hf * P : (hf + 1) * P],
                            rhs=ident[:],
                            is_transpose=True,
                            start=(q == 0),
                            stop=(q == 3),
                        )
                ps1s[k][hf] = ps1

        def round_sum(k):
            g = ITEMS[k][1]
            p_t = tpool.tile([P, 2, 2, P, 2], BF16, name="p_t", align_bytes=256)
            pts[k] = p_t
            for hf in halves(k, "P"):
                sums = ps1s[k][hf][:].rearrange("p (u e) c -> p u c e", e=2)
                nc.vector.tensor_tensor(out=p_t[:, hf], in0=sums, in1=cst[:, g], op=ALU.add)

        def turn_back(k):
            ps2 = psum.tile([P, 2, 2 * P], F32, name="ps2", tag="bank")
            ptw = pts[k][:].rearrange("p h u c e -> p h u (c e)").bitcast(F32)
            for hf in halves(k, "P"):
                for u in range(2):
                    nc.tensor.transpose(ps2[:, u, hf * P : (hf + 1) * P], ptw[:, hf, u, :], ident[:])
            ps2s[k] = ps2

        def g_tile(k):
            if k not in grps:
                grps[k] = gpool.tile([P, ITEMS[k][3], 4], BF16, name="grp", align_bytes=256)
            return grps[k]

        def copy_back(k):
            hs_p = halves(k, "P")
            lo, hi = hs_p[0] * P, (hs_p[-1] + 1) * P
            nc.scalar.copy(out=g_tile(k)[:, lo:hi, :].bitcast(F32), in_=ps2s[k][:, :, lo:hi].rearrange("p u x -> p x u"))

        def v_run(k):
            return slice(halves(k, "V")[0] * P, (halves(k, "V")[-1] + 1) * P)

        def add_cols(k):
            r = rs[k]
            px = v_run(k)
            h = hpool.tile([P, 2, 4, px.stop - px.start], F32, name="h", align_bytes=256)
            hs[k] = h
            for t in range(4) if k == n_items - 1 else reversed(range(4)):
                col = 4 * ITEMS[k][1] + t
                nc.vector.scalar_tensor_tensor(
                    out=h[:, :, t, :],
                    in0=r[:, :, 0, t, px],
                    scalar=sh4[:, col : col + 1] if t < 4 - S_EXTRA[k] else 0.0,
                    in1=r[:, :, 1, t, px],
                    op0=ALU.add,
                    op1=ALU.add,
                )

        def add_rows(k):
            h = hs[k]
            nc.vector.tensor_tensor(
                out=g_tile(k)[:, v_run(k), :].rearrange("p (c i) t -> p c t i", i=4),
                in0=h[:, 0].rearrange("p t (c i) -> p c t i", i=4),
                in1=h[:, 1].rearrange("p t (c i) -> p c t i", i=4),
                op=ALU.add,
            )

        def mx_pass(acc_ap, bt, g, m, p0, npx, start, stop):
            codes, scl = cds[bt]
            nc.tensor.matmul_mx(
                out=acc_ap,
                lhsT=wcodes[:, g * MT + m, :].bitcast(FP8X4),
                lhsT_scale=wsc[:, g * MT + m, :],
                rhs=codes[:, g, p0 : p0 + npx].bitcast(FP8X4),
                rhs_scale=scl[:, g, p0 : p0 + npx],
                start=start,
                stop=stop,
            )

        quantised = set()

        def quant(k):
            bt, g, p0, npx = ITEMS[k]
            if bt not in cds:
                codes = cpool.tile([P, PASSES, PIX], U32, name="codes", align_bytes=256)
                scl = cpool.tile([P, PASSES, PIX], U8, name="scl", align_bytes=256)
                cds[bt] = (codes, scl)
            codes, scl = cds[bt]
            nc.vector.quantize_mx(
                out=codes[:, g, p0 : p0 + npx].bitcast(FP8X4),
                scales=scl[:, g, p0 : p0 + npx],
                in_=grps[k][:].rearrange("p x t -> p (x t)"),
            )
            quantised.add(k)
            if k >= n_items - PASSES:
                first = (bt, p0) not in accs
                if first:
                    accs[(bt, p0)] = [psum.tile([P, npx], F32, name="acc%d" % m, tag="bank") for m in range(MT)]
                for m in range(MT):
                    mx_pass(accs[(bt, p0)][m][:], bt, g, m, p0, npx, first, not first)

        def conv(k):
            bt, g, p0, npx = ITEMS[k]
            per_bank = 512 // npx
            banks = []
            for j in range(MT // per_bank):
                acc = psum.tile([P, per_bank, npx], F32, name="acc", tag="bank")
                for e in range(per_bank):
                    for gg in range(PASSES):
                        mx_pass(acc[:, e, :], bt, gg, j * per_bank + e, p0, npx, gg == 0, gg == PASSES - 1)
                banks.append(acc)
            accs[(bt, p0)] = banks

        def evacuate(k):
            bt, g, p0, npx = ITEMS[k]
            if bt not in osbs:
                osbs[bt] = opool.tile([P, MT, PIX], F32, name="o_sb", align_bytes=256)
            o_sb = osbs[bt]
            banks = accs[(bt, p0)]
            dst = out[bt].rearrange("(o m) h w -> o m (h w)", o=P)
            per_bank = MT // len(banks)
            if k == n_items - 1:
                for m in range(MT):
                    if m < MT // 2:
                        nc.scalar.copy(out=o_sb[:, m, p0 : p0 + npx], in_=banks[m][:])
                    else:
                        nc.vector.tensor_copy(out=o_sb[:, m, p0 : p0 + npx], in_=banks[m][:])
                for j in range(2):
                    nc.sync.dma_start(
                        out=dst[:, 2 * j : 2 * j + 2, p0 : p0 + npx], in_=o_sb[:, 2 * j : 2 * j + 2, p0 : p0 + npx]
                    )
            else:
                for j in range(len(banks)):
                    dst_sb = o_sb[:, j * per_bank : (j + 1) * per_bank, p0 : p0 + npx]
                    if k == n_items - 3:
                        nc.vector.tensor_copy(out=dst_sb, in_=banks[j][:])
                    else:
                        nc.scalar.copy(out=dst_sb, in_=banks[j][:])
                    if k >= SPLIT_STORE:
                        ms = slice(j * per_bank, (j + 1) * per_bank)
                        nc.sync.dma_start(out=dst[:, ms, p0 : p0 + npx], in_=o_sb[:, ms, p0 : p0 + npx])
                if k < SPLIT_STORE:
                    nc.sync.dma_start(out=dst[:, :, p0 : p0 + npx], in_=o_sb[:, :, p0 : p0 + npx])

        last_item_of_chunk = {}
        for k in range(n_items):
            last_item_of_chunk[ITEMS[k][0] * PASSES + ITEMS[k][1]] = k
        closers = [k for k in range(n_items - PASSES) if ITEMS[k][1] == PASSES - 1]
        conv_step = {}
        evac_done = set()

        shift_rows_pe()
        for k in range(AHEAD):
            affine_v(k)
        if not CST_ON_SCALAR:
            shift_rows_copy()
        quant_step = {}
        for j in range(n_items):
            if j == W_COPY_STEP and W_FIRST:
                weight_copies()
            affine_s(j)
            if CST_ON_SCALAR and j == 0:
                shift_rows_copy()
            c = ITEMS[j][0] * PASSES + ITEMS[j][1]
            if last_item_of_chunk[c] == j and c + XB < B * PASSES:
                load(c + XB)
            if j == W_COPY_STEP and not W_FIRST:
                weight_copies()
            if j == W_T_STEP:
                weight_transposes()
            for k in due(j, L_ROUND, "P"):
                round_sum(k)
            for k in due(j, L_SUM, "P"):
                sum_planes(k)
            for k in due(j, L_TURN, "P"):
                turn_back(k)
            for k in due(j, L_BACK, "P"):
                copy_back(k)
            for k in closers:
                if k in conv_step and k not in evac_done and j > conv_step[k]:
                    evacuate(k)
                    evac_done.add(k)
            for k in due(j, 1, "V"):
                add_cols(k)
            for k in due(j, L_QP, "P"):
                quant(k)
                quant_step[k] = j
            if AHEAD == 2:
                affine_v(j + 2)
            for k in due(j, L_QV, "V"):
                if not halves(k, "P"):
                    quant(k)
                    quant_step[k] = j
            for k in due(j, 1, "V"):
                add_rows(k)
            if AHEAD == 1:
                affine_v(j + 1)
            if j == W_COPY_STEP:
                weight_quant()
            if j >= W_COPY_STEP:
                for k in closers:
                    if k not in conv_step and k in quantised and (k - 1) in quantised:
                        if quant_step[k] < j + (k >= SAME_STEP) and quant_step[k - 1] < j and j not in conv_step.values():
                            conv(k)
                            conv_step[k] = j
        turn_back(15)
        copy_back(14)
        evacuate(11)
        quant(13)
        round_sum(16)
        copy_back(15)
        turn_back(16)
        conv(13)
        copy_back(16)
        quant(14)
        add_cols(17)
        quant(15)
        evacuate(13)
        conv(15)
        add_rows(17)
        quant(16)
        quant(17)
        evacuate(15)
        evacuate(17)
